import numpy as np
import ml_dtypes


def mxq(x, axis, fmt="e4m3"):
    dtype, down = {"e4m3": (ml_dtypes.float8_e4m3fn, 7), "e5m2": (ml_dtypes.float8_e5m2, 14)}[fmt]
    v = np.moveaxis(np.asarray(x, np.float32).astype(ml_dtypes.bfloat16).astype(np.float64), axis, -1)
    blocks = v.reshape(v.shape[:-1] + (-1, 32))
    amax = np.abs(blocks).max(-1, keepdims=True)
    byte = np.maximum(np.where(amax > 0, np.frexp(amax)[1] - 1 + 127, 0) - down, 1)
    scale = np.exp2(byte - 127.0)
    codes = (blocks / scale).astype(np.float32).astype(dtype).astype(np.float64)
    return np.moveaxis((codes * scale).reshape(v.shape), -1, axis)


WIDE = False


def mx_kscale(k):
    if not WIDE:
        return np.ones(k)
    levels = np.array([20, -20, 10, -10, 0])
    a = np.random.permutation(np.resize(levels, k // 512 * 4)).reshape(k // 512, 4)
    idx = np.arange(k)
    return np.exp2(a[idx // 512, idx % 128 // 32])


BF16 = ml_dtypes.bfloat16


def bf(x):
    return np.asarray(x, np.float32).astype(BF16)


def f64(x):
    return np.asarray(x).astype(np.float64)


B, C, K, H, W = 2, 512, 512, 64, 64
N = H * W


def setup_inputs():
    u = mx_kscale(C)[None, :, None]
    feats = np.random.standard_normal((B, C, N)) * 4.0 / u
    probs = np.random.standard_normal((B, K, N)) * 2.0
    g = np.random.standard_normal((B, C, K)) * np.exp2(np.random.randint(-12, 1, (B, 1, K))) * 16.0 * u
    return {"feats": bf(feats.reshape(B, C, H, W)), "probs": bf(probs.reshape(B, K, H, W)),
            "grad_out": bf(g.reshape(B, C, K, 1))}


def reference(feats, probs, grad_out):
    x = f64(feats).reshape(B, C, N)
    l = f64(probs).reshape(B, K, N)
    g = f64(grad_out).reshape(B, C, K)
    e = np.exp(l - l.max(2, keepdims=True))
    p = e / e.sum(2, keepdims=True)
    gp = mxq(g, 1, "e5m2").transpose(0, 2, 1) @ mxq(x, 1, "e4m3")
    d = (p * gp).sum(2, keepdims=True)
    return (p * (gp - d)).reshape(B, K, H, W)

@@ -1,0 +1,224 @@
+from contextlib import ExitStack
+
+import concourse.mybir as mybir
+
+FLOPS = 2 * 2 * 512 * 512 * 4096
+
+F32 = mybir.dt.float32
+BF16 = mybir.dt.bfloat16
+U32 = mybir.dt.uint32
+U8 = mybir.dt.uint8
+E4X4 = mybir.dt.float8_e4m3fn_x4
+E5X4 = mybir.dt.float8_e5m2_x4
+ALU = mybir.AluOpType
+ACT = mybir.ActivationFunctionType
+AXIS = mybir.AxisListType
+
+P = 128
+PACK = 4
+B = 2
+K = 512
+N = 4096
+KT = K // P
+NT = B * KT
+CH = 1024
+NCH = N // CH
+BANK = 512
+NB = N // BANK
+VCOLS = 2048
+GSTEP = 512
+
+
+def build_order():
+    seq = []
+    seq += [("ld_raw", 0), ("ld_l", 0), ("ld_raw", 1), ("ld_raw", 2), ("ld_l", 1), ("ld_raw", 3)]
+    seq += [("warm",), ("rg", 0, "v"), ("mx", 0), ("q", 0), ("ld_raw", 4), ("ex", 0)]
+    seq += [("rg", 1, "v"), ("rg", 2, "s"), ("mx", 1), ("q", 1), ("ld_l", 2), ("ld_raw", 5), ("rc", 0)]
+    seq += [("mm", 0, 0), ("mm", 0, 1), ("p1", 0, 0), ("p1", 0, 1), ("q", 2), ("ld_raw", 6), ("ex", 1)]
+    seq += [("mm", 0, 2), ("mm", 0, 3), ("p1", 0, 2), ("p1", 0, 3)]
+    seq += [("rg", 3, "v"), ("rg", 4, "s"), ("mx", 2), ("q", 3), ("ld_l", 3), ("ld_raw", 7)]
+    seq += [("mm", 0, 4), ("mm", 0, 5), ("p1", 0, 4), ("p1", 0, 5), ("q", 4), ("ld_raw", 8), ("ex", 2)]
+    seq += [("mm", 0, 6), ("mm", 0, 7), ("p1", 0, 6), ("p1", 0, 7)]
+    seq += [("ds", 0), ("rc", 1), ("c2", 0)]
+    for t in range(NT):
+        seq += [("u", t), ("p2v", t), ("st", t, 0)]
+        if t < NCH:
+            seq += [("rg", 5 + t, "s")]
+        if t + 4 < NT:
+            seq += [("ld_l", t + 4)]
+        if t + 3 < NT:
+            seq += [("mx", t + 3), ("ex", t + 3)]
+        if t < NCH:
+            seq += [("q", 5 + t)]
+        if t + 1 < NT:
+            seq += [("mm", t + 1, j) for j in range(NB)]
+            seq += [("p1", t + 1, j) for j in range(NB)]
+        seq += [("p2g", t), ("st", t, 1)]
+        if t + 1 < NT:
+            seq += [("ds", t + 1)]
+            if t + 2 < NT:
+                seq += [("rc", t + 2)]
+            seq += [("c2", t + 1)]
+    return seq
+
+
+def tile_spatialgather_module_kernel(tc, feats, probs, grad_out, out):
+    nc = tc.nc
+    x_v = feats.rearrange("b (p j) h w -> b p j (h w)", j=PACK)
+    g_v = grad_out.rearrange("b (p j) k o -> p b j (k o)", j=PACK)
+    l_v = probs.rearrange("b (t p) h w -> b t p (h w)", p=P)
+    o_v = out.rearrange("b (t p) h w -> b t p (h w)", p=P)
+
+    with ExitStack() as ctx:
+        rawp = ctx.enter_context(tc.tile_pool(name="rawp", bufs=4))
+        grpp = ctx.enter_context(tc.tile_pool(name="grpp", bufs=2))
+        keep = ctx.enter_context(tc.tile_pool(name="keep", bufs=1))
+        lpool = ctx.enter_context(tc.tile_pool(name="lpool", bufs=4))
+        epool = ctx.enter_context(tc.tile_pool(name="epool", bufs=3))
+        tpool = ctx.enter_context(tc.tile_pool(name="tpool", bufs=3))
+        small = ctx.enter_context(tc.tile_pool(name="small", bufs=4))
+        psum = ctx.enter_context(tc.psum_pool(name="psum", bufs=8))
+
+        g_codes = keep.tile([P, B * K], U32, name="g_codes", align_bytes=64)
+        g_scales = keep.tile([P, B * K], U8, name="g_scales", align_bytes=64)
+        x_codes = [keep.tile([P, N], U32, name="x_codes%d" % b, align_bytes=64) for b in range(B)]
+        x_scales = [keep.tile([P, N], U8, name="x_scales%d" % b, align_bytes=64) for b in range(B)]
+
+        raw = {}
+        grp = {}
+        lt = {}
+        et = {}
+        tt = {}
+        ps = {}
+        negm = {}
+        ssum = {}
+        rs = {}
+        dparts = {}
+        dsum = {}
+        c2 = {}
+
+        def ld_raw(i):
+            if i == 0:
+                raw[i] = rawp.tile([P, B, PACK, K], BF16, name="raw", tag="raw")
+                nc.sync.dma_start(out=raw[i][:], in_=g_v)
+            else:
+                b, c = divmod(i - 1, NCH)
+                raw[i] = rawp.tile([P, PACK, CH], BF16, name="raw", tag="raw")
+                nc.sync.dma_start(out=raw[i][:], in_=x_v[b, :, :, c * CH : (c + 1) * CH])
+
+        def ld_l(t):
+            b, kt = divmod(t, KT)
+            lt[t] = lpool.tile([P, N], BF16, name="lt", tag="lt")
+            nc.sync.dma_start(out=lt[t][:], in_=l_v[b, kt])
+
+        def warm():
+            w0 = small.tile([P, 1], F32, name="w0", tag="w0")
+            w1 = small.tile([P, 1], F32, name="w1", tag="w1")
+            nc.vector.memset(w0[:], 0.0)
+            nc.scalar.activation(out=w1[:], in_=w0[:], func=ACT.Exp)
+
+        def rg(i, eng):
+            copy = nc.vector.tensor_copy if eng == "v" else nc.scalar.copy
+            grp[i] = grpp.tile([P, CH, PACK], BF16, name="grp", tag="grp", align_bytes=64)
+            if i == 0:
+                pairs = [(grp[i][:, b * K : (b + 1) * K, :], raw[i][:, b]) for b in range(B)]
+            else:
+                pairs = [(grp[i][:], raw[i][:])]
+            for dst, src in pairs:
+                copy(
+                    out=dst.rearrange("p (c i) t -> p c t i", i=4),
+                    in_=src.rearrange("p t (c i) -> p c t i", i=4),
+                )
+
+        def q(i):
+            if i == 0:
+                codes = g_codes[:].bitcast(E5X4)
+                scales = g_scales[:]
+            else:
+                b, c = divmod(i - 1, NCH)
+                codes = x_codes[b][:, c * CH : (c + 1) * CH].bitcast(E4X4)
+                scales = x_scales[b][:, c * CH : (c + 1) * CH]
+            nc.vector.quantize_mx(out=codes, scales=scales, in_=grp[i][:].rearrange("p w j -> p (w j)"))
+
+        def mx(t):
+            negm[t] = small.tile([P, 1], F32, name="negm", tag="negm")
+            nc.vector.tensor_scalar(
+                out=lt[t][:], in0=lt[t][:], scalar1=-1.0, scalar2=None,
+                op0=ALU.mult, op1=ALU.min, accum_out=negm[t][:],
+            )
+
+        def ex(t):
+            et[t] = epool.tile([P, N], F32, name="et", tag="et")
+            ssum[t] = small.tile([P, 1], F32, name="ssum", tag="ssum")
+            nc.scalar.activation(
+                out=et[t][:], in_=lt[t][:], func=ACT.Exp, bias=negm[t][:], scale=-1.0, accum_out=ssum[t][:],
+            )
+
+        def rc(t):
+            rs[t] = small.tile([P, 1], F32, name="rs", tag="rs")
+            nc.vector.reciprocal(out=rs[t][:], in_=ssum[t][:])
+
+        def mm(t, j):
+            b, kt = divmod(t, KT)
+            ps[(t, j)] = psum.tile([P, BANK], F32, name="ps", tag="ps")
+            gcols = slice(b * K + kt * P, b * K + (kt + 1) * P)
+            xcols = slice(j * BANK, (j + 1) * BANK)
+            nc.tensor.matmul_mx(
+                out=ps[(t, j)][:],
+                lhsT=g_codes[:, gcols].bitcast(E5X4),
+                lhsT_scale=g_scales[:, gcols],
+                rhs=x_codes[b][:, xcols].bitcast(E4X4),
+                rhs_scale=x_scales[b][:, xcols],
+                start=True,
+                stop=True,
+            )
+
+        def p1(t, j):
+            if j == 0:
+                tt[t] = tpool.tile([P, N], F32, name="tt", tag="tt")
+                dparts[t] = small.tile([P, NB], F32, name="dparts", tag="dparts")
+            cols = slice(j * BANK, (j + 1) * BANK)
+            nc.vector.scalar_tensor_tensor(
+                out=tt[t][:, cols], in0=ps[(t, j)][:], scalar=rs[t][:], in1=et[t][:, cols],
+                op0=ALU.mult, op1=ALU.mult, accum_out=dparts[t][:, j : j + 1],
+            )
+
+        def ds(t):
+            dsum[t] = small.tile([P, 1], F32, name="dsum", tag="dsum")
+            nc.vector.tensor_reduce(out=dsum[t][:], in_=dparts[t][:], axis=AXIS.X, op=ALU.add)
+
+        def c2f(t):
+            c2[t] = small.tile([P, 1], F32, name="c2", tag="c2")
+            nc.vector.tensor_scalar(
+                out=c2[t][:], in0=dsum[t][:], scalar1=rs[t][:], scalar2=-1.0, op0=ALU.mult, op1=ALU.mult,
+            )
+
+        def p2v(t):
+            cols = slice(0, VCOLS)
+            nc.vector.scalar_tensor_tensor(
+                out=tt[t][:, cols], in0=et[t][:, cols], scalar=c2[t][:], in1=tt[t][:, cols],
+                op0=ALU.mult, op1=ALU.add,
+            )
+
+        def u(t):
+            for c0 in range(VCOLS, N, GSTEP):
+                cols = slice(c0, c0 + GSTEP)
+                nc.scalar.activation(out=et[t][:, cols], in_=et[t][:, cols], func=ACT.Copy, scale=c2[t][:])
+
+        def p2g(t):
+            for c0 in range(VCOLS, N, GSTEP):
+                cols = slice(c0, c0 + GSTEP)
+                nc.gpsimd.tensor_tensor(out=tt[t][:, cols], in0=tt[t][:, cols], in1=et[t][:, cols], op=ALU.add)
+
+        def st(t, h):
+            b, kt = divmod(t, KT)
+            cols = slice(0, VCOLS) if h == 0 else slice(VCOLS, N)
+            nc.sync.dma_start(out=o_v[b, kt][:, cols], in_=tt[t][:, cols])
+
+        ops = {
+            "ld_raw": ld_raw, "ld_l": ld_l, "warm": warm, "rg": rg, "q": q, "mx": mx, "ex": ex, "rc": rc,
+            "mm": mm, "p1": p1, "ds": ds, "c2": c2f, "p2v": p2v, "u": u, "p2g": p2g, "st": st,
+        }
+        with tc.manual_schedule():
+            for step in build_order():
+                ops[step[0]](*step[1:])

@@ -25,31 +25,30 @@ CH = 1024
 NCH = N // CH
 BANK = 512
 NB = N // BANK
-VCOLS = 2048
 GSTEP = 512
+USTEP = 1024
+ITEMS = [("g", 0, 0), ("x", 0, 0), ("x", 0, 1), ("x", 0, 2), ("x", 0, 3), ("g", 1, 0), ("x", 1, 0), ("x", 1, 1), ("x", 1, 2), ("x", 1, 3)]
+VCOLS = [2048, 2048, 2048, 2048, 2048, 2048, 2048, 4096]
 
 
 def build_order():
     seq = []
-    seq += [("ld_raw", 0), ("ld_l", 0), ("ld_raw", 1), ("ld_raw", 2), ("ld_l", 1), ("ld_raw", 3)]
-    seq += [("warm",), ("rg", 0, "v"), ("mx", 0), ("q", 0), ("ld_raw", 4), ("ex", 0)]
-    seq += [("rg", 1, "v"), ("rg", 2, "s"), ("mx", 1), ("q", 1), ("ld_l", 2), ("ld_raw", 5), ("rc", 0)]
-    seq += [("mm", 0, 0), ("mm", 0, 1), ("p1", 0, 0), ("p1", 0, 1), ("q", 2), ("ld_raw", 6), ("ex", 1)]
-    seq += [("mm", 0, 2), ("mm", 0, 3), ("p1", 0, 2), ("p1", 0, 3)]
-    seq += [("rg", 3, "v"), ("rg", 4, "s"), ("mx", 2), ("q", 3), ("ld_l", 3), ("ld_raw", 7)]
-    seq += [("mm", 0, 4), ("mm", 0, 5), ("p1", 0, 4), ("p1", 0, 5), ("q", 4), ("ld_raw", 8), ("ex", 2)]
-    seq += [("mm", 0, 6), ("mm", 0, 7), ("p1", 0, 6), ("p1", 0, 7)]
+    seq += [("ld_raw", 0), ("ld_l", 0), ("ld_raw", 1), ("ld_raw", 2), ("ld_raw", 3), ("warm",)]
+    seq += [("rg", 0, "v"), ("ld_raw", 4), ("ld_l", 1), ("mx", 0), ("ex", 0), ("q", 0)]
+    seq += [("rg", 1, "v"), ("ld_raw", 6), ("ld_l", 2), ("rg", 2, "v"), ("ld_raw", 7), ("q", 1), ("rg", 3, "s"), ("ld_raw", 5), ("q", 2), ("rc", 0)]
+    seq += [("mm", 0, 0), ("mm", 0, 1), ("mm", 0, 2), ("mm", 0, 3), ("p1", 0, 0), ("p1", 0, 1)]
+    seq += [("rg", 4, "v"), ("ld_l", 3), ("ld_raw", 8), ("mx", 1), ("rg", 6, "s"), ("ex", 1), ("p1", 0, 2), ("p1", 0, 3), ("q", 3), ("q", 4)]
+    seq += [("mm", 0, 4), ("mm", 0, 5), ("mm", 0, 6), ("mm", 0, 7)]
+    seq += [("mx", 2), ("p1", 0, 4), ("p1", 0, 5), ("p1", 0, 6), ("p1", 0, 7)]
     seq += [("ds", 0), ("rc", 1), ("c2", 0)]
+    s_extra = {0: [("rg", 7, "s"), ("ex", 2)], 1: [("rg", 8, "s"), ("ex", 3)], 2: [("rg", 9, "s"), ("ex", 4)], 3: [("ex", 5)], 4: [("ex", 6)], 5: [("ex", 7)]}
+    v_extra = {0: [("rg", 5, "v"), ("q", 6), ("mx", 3), ("q", 5)], 1: [("q", 7), ("mx", 4)], 2: [("q", 8), ("mx", 5)], 3: [("q", 9), ("mx", 6)], 4: [("mx", 7)]}
+    l_extra = {0: [("ld_raw", 9), ("ld_l", 4)], 1: [("ld_l", 5)], 2: [("ld_l", 6)], 3: [("ld_l", 7)]}
     for t in range(NT):
         seq += [("u", t), ("p2v", t), ("st", t, 0)]
-        if t < NCH:
-            seq += [("rg", 5 + t, "s")]
-        if t + 4 < NT:
-            seq += [("ld_l", t + 4)]
-        if t + 3 < NT:
-            seq += [("mx", t + 3), ("ex", t + 3)]
-        if t < NCH:
-            seq += [("q", 5 + t)]
+        seq += l_extra.get(t, [])
+        seq += s_extra.get(t, [])
+        seq += v_extra.get(t, [])
         if t + 1 < NT:
             seq += [("mm", t + 1, j) for j in range(NB)]
             seq += [("p1", t + 1, j) for j in range(NB)]
@@ -71,7 +70,7 @@ def tile_spatialgather_module_kernel(tc, feats, probs, grad_out, out):
 
     with ExitStack() as ctx:
         rawp = ctx.enter_context(tc.tile_pool(name="rawp", bufs=4))
-        grpp = ctx.enter_context(tc.tile_pool(name="grpp", bufs=2))
+        grpp = ctx.enter_context(tc.tile_pool(name="grpp", bufs=3))
         keep = ctx.enter_context(tc.tile_pool(name="keep", bufs=1))
         lpool = ctx.enter_context(tc.tile_pool(name="lpool", bufs=4))
         epool = ctx.enter_context(tc.tile_pool(name="epool", bufs=3))
@@ -98,11 +97,11 @@ def tile_spatialgather_module_kernel(tc, feats, probs, grad_out, out):
         c2 = {}
 
         def ld_raw(i):
-            if i == 0:
-                raw[i] = rawp.tile([P, B, PACK, K], BF16, name="raw", tag="raw")
-                nc.sync.dma_start(out=raw[i][:], in_=g_v)
+            kind, b, c = ITEMS[i]
+            if kind == "g":
+                raw[i] = rawp.tile([P, PACK, K], BF16, name="raw", tag="raw")
+                nc.sync.dma_start(out=raw[i][:], in_=g_v[:, b])
             else:
-                b, c = divmod(i - 1, NCH)
                 raw[i] = rawp.tile([P, PACK, CH], BF16, name="raw", tag="raw")
                 nc.sync.dma_start(out=raw[i][:], in_=x_v[b, :, :, c * CH : (c + 1) * CH])
 
@@ -119,23 +118,19 @@ def tile_spatialgather_module_kernel(tc, feats, probs, grad_out, out):
 
         def rg(i, eng):
             copy = nc.vector.tensor_copy if eng == "v" else nc.scalar.copy
-            grp[i] = grpp.tile([P, CH, PACK], BF16, name="grp", tag="grp", align_bytes=64)
-            if i == 0:
-                pairs = [(grp[i][:, b * K : (b + 1) * K, :], raw[i][:, b]) for b in range(B)]
-            else:
-                pairs = [(grp[i][:], raw[i][:])]
-            for dst, src in pairs:
-                copy(
-                    out=dst.rearrange("p (c i) t -> p c t i", i=4),
-                    in_=src.rearrange("p t (c i) -> p c t i", i=4),
-                )
+            width = K if ITEMS[i][0] == "g" else CH
+            grp[i] = grpp.tile([P, width, PACK], BF16, name="grp", tag="grp", align_bytes=64)
+            copy(
+                out=grp[i][:].rearrange("p (c i) t -> p c t i", i=4),
+                in_=raw[i][:].rearrange("p t (c i) -> p c t i", i=4),
+            )
 
         def q(i):
-            if i == 0:
-                codes = g_codes[:].bitcast(E5X4)
-                scales = g_scales[:]
+            kind, b, c = ITEMS[i]
+            if kind == "g":
+                codes = g_codes[:, b * K : (b + 1) * K].bitcast(E5X4)
+                scales = g_scales[:, b * K : (b + 1) * K]
             else:
-                b, c = divmod(i - 1, NCH)
                 codes = x_codes[b][:, c * CH : (c + 1) * CH].bitcast(E4X4)
                 scales = x_scales[b][:, c * CH : (c + 1) * CH]
             nc.vector.quantize_mx(out=codes, scales=scales, in_=grp[i][:].rearrange("p w j -> p (w j)"))
@@ -194,26 +189,32 @@ def tile_spatialgather_module_kernel(tc, feats, probs, grad_out, out):
             )
 
         def p2v(t):
-            cols = slice(0, VCOLS)
-            nc.vector.scalar_tensor_tensor(
-                out=tt[t][:, cols], in0=et[t][:, cols], scalar=c2[t][:], in1=tt[t][:, cols],
-                op0=ALU.mult, op1=ALU.add,
-            )
+            step = VCOLS[t] if VCOLS[t] < N else CH
+            for c0 in range(0, VCOLS[t], step):
+                cols = slice(c0, c0 + step)
+                nc.vector.scalar_tensor_tensor(
+                    out=tt[t][:, cols], in0=et[t][:, cols], scalar=c2[t][:], in1=tt[t][:, cols],
+                    op0=ALU.mult, op1=ALU.add,
+                )
 
         def u(t):
-            for c0 in range(VCOLS, N, GSTEP):
-                cols = slice(c0, c0 + GSTEP)
+            for c0 in range(VCOLS[t], N, USTEP):
+                cols = slice(c0, c0 + USTEP)
                 nc.scalar.activation(out=et[t][:, cols], in_=et[t][:, cols], func=ACT.Copy, scale=c2[t][:])
 
         def p2g(t):
-            for c0 in range(VCOLS, N, GSTEP):
+            for c0 in range(VCOLS[t], N, GSTEP):
                 cols = slice(c0, c0 + GSTEP)
                 nc.gpsimd.tensor_tensor(out=tt[t][:, cols], in0=tt[t][:, cols], in1=et[t][:, cols], op=ALU.add)
 
         def st(t, h):
             b, kt = divmod(t, KT)
-            cols = slice(0, VCOLS) if h == 0 else slice(VCOLS, N)
-            nc.sync.dma_start(out=o_v[b, kt][:, cols], in_=tt[t][:, cols])
+            if VCOLS[t] < N:
+                parts = [slice(0, VCOLS[t])] if h == 0 else [slice(VCOLS[t], N)]
+            else:
+                parts = [slice(c0, c0 + CH) for c0 in range(0, N, CH)] if h == 0 else []
+            for cols in parts:
+                nc.sync.dma_start(out=o_v[b, kt][:, cols], in_=tt[t][:, cols])
 
         ops = {
             "ld_raw": ld_raw, "ld_l": ld_l, "warm": warm, "rg": rg, "q": q, "mx": mx, "ex": ex, "rc": rc,

@@ -33,31 +33,30 @@ VCOLS = [2048, 2048, 2048, 2048, 2048, 2048, 2048, 4096]
 
 def build_order():
     seq = []
-    seq += [("ld_raw", 0), ("ld_l", 0), ("ld_raw", 1), ("ld_raw", 2), ("ld_raw", 3), ("warm",)]
-    seq += [("rg", 0, "v"), ("ld_raw", 4), ("ld_l", 1), ("mx", 0), ("ex", 0), ("q", 0)]
-    seq += [("rg", 1, "v"), ("ld_raw", 6), ("ld_l", 2), ("rg", 2, "v"), ("ld_raw", 7), ("q", 1), ("rg", 3, "s"), ("ld_raw", 5), ("q", 2), ("rc", 0)]
-    seq += [("mm", 0, 0), ("mm", 0, 1), ("mm", 0, 2), ("mm", 0, 3), ("p1", 0, 0), ("p1", 0, 1)]
-    seq += [("rg", 4, "v"), ("ld_l", 3), ("ld_raw", 8), ("mx", 1), ("rg", 6, "s"), ("ex", 1), ("p1", 0, 2), ("p1", 0, 3), ("q", 3), ("q", 4)]
-    seq += [("mm", 0, 4), ("mm", 0, 5), ("mm", 0, 6), ("mm", 0, 7)]
-    seq += [("mx", 2), ("p1", 0, 4), ("p1", 0, 5), ("p1", 0, 6), ("p1", 0, 7)]
-    seq += [("ds", 0), ("rc", 1), ("c2", 0)]
-    s_extra = {0: [("rg", 7, "s"), ("ex", 2)], 1: [("rg", 8, "s"), ("ex", 3)], 2: [("rg", 9, "s"), ("ex", 4)], 3: [("ex", 5)], 4: [("ex", 6)], 5: [("ex", 7)]}
-    v_extra = {0: [("rg", 5, "v"), ("q", 6), ("mx", 3), ("q", 5)], 1: [("q", 7), ("mx", 4)], 2: [("q", 8), ("mx", 5)], 3: [("q", 9), ("mx", 6)], 4: [("mx", 7)]}
-    l_extra = {0: [("ld_raw", 9), ("ld_l", 4)], 1: [("ld_l", 5)], 2: [("ld_l", 6)], 3: [("ld_l", 7)]}
+    seq += [("ld_l", 0), ("ld_raw", 0), ("ld_raw", 1), ("ld_raw", 2), ("ld_raw", 4), ("warm",)]
+    seq += [("mx", 0), ("ex", 0), ("rg", 0, "v"), ("ld_raw", 3), ("ld_l", 1), ("ld_l", 2), ("ld_l", 3), ("q", 0), ("rg", 1, "v"), ("ld_raw", 6), ("ld_l", 4), ("q", 1), ("rc", 0)]
+    seq += [("mm", 0, 0), ("mm", 0, 1), ("p1", 0, 0), ("rg", 2, "s"), ("rg", 4, "v"), ("ld_raw", 5), ("p1", 0, 1), ("q", 4), ("q", 2), ("ld_raw", 7)]
+    seq += [("mm", 0, 6), ("mm", 0, 7), ("mm", 0, 2), ("mm", 0, 3), ("rg", 3, "s"), ("ld_raw", 8), ("mx", 1), ("ex", 1), ("ld_l", 5), ("mx", 2), ("q", 3), ("mm", 0, 4), ("mm", 0, 5)]
+    seq += [("p1", 0, 2), ("p1", 0, 3), ("mx", 3), ("p1", 0, 4), ("p1", 0, 5), ("p1", 0, 6), ("p1", 0, 7)]
+    seq += [("rg", 6, "s"), ("rg", 5, "s"), ("ld_raw", 9), ("ds", 0), ("c2", 0)]
+    s_extra = {0: [("ex", 2), ("rg", 7, "s")], 1: [("ex", 3), ("rg", 8, "s")], 2: [("ex", 4), ("rg", 9, "s")], 3: [("ex", 5)], 4: [("ex", 6)], 5: [("ex", 7)]}
+    v_extra = {0: [("mx", 4)], 1: [("mx", 5)], 2: [("mx", 6), ("q", 5)], 3: [("mx", 7)]}
+    v_late = {0: [("q", 6)], 1: [("q", 7)], 2: [("q", 8)], 3: [("q", 9)]}
+    l_extra = {0: [("ld_l", 6)], 1: [("ld_l", 7)]}
     for t in range(NT):
-        seq += [("u", t), ("p2v", t), ("st", t, 0)]
+        seq += [("u", t)]
         seq += l_extra.get(t, [])
         seq += s_extra.get(t, [])
         seq += v_extra.get(t, [])
+        seq += [("p2v", t), ("st", t, 0)]
+        seq += v_late.get(t, [])
         if t + 1 < NT:
+            seq += [("rc", t + 1)]
             seq += [("mm", t + 1, j) for j in range(NB)]
             seq += [("p1", t + 1, j) for j in range(NB)]
         seq += [("p2g", t), ("st", t, 1)]
         if t + 1 < NT:
-            seq += [("ds", t + 1)]
-            if t + 2 < NT:
-                seq += [("rc", t + 2)]
-            seq += [("c2", t + 1)]
+            seq += [("ds", t + 1), ("c2", t + 1)]
     return seq
 
 

@@ -26,37 +26,40 @@ NCH = N // CH
 BANK = 512
 NB = N // BANK
 GSTEP = 512
-USTEP = 1024
+USTEP = 512
+VPIECES = [(0, 768), (768, 1408), (1408, 2048)]
 ITEMS = [("g", 0, 0), ("x", 0, 0), ("x", 0, 1), ("x", 0, 2), ("x", 0, 3), ("g", 1, 0), ("x", 1, 0), ("x", 1, 1), ("x", 1, 2), ("x", 1, 3)]
 VCOLS = [2048, 2048, 2048, 2048, 2048, 2048, 2048, 4096]
 
 
 def build_order():
     seq = []
-    seq += [("ld_l", 0), ("ld_raw", 0), ("ld_raw", 1), ("ld_raw", 2), ("ld_raw", 4), ("warm",)]
-    seq += [("mx", 0), ("ex", 0), ("rg", 0, "v"), ("ld_raw", 3), ("ld_l", 1), ("ld_l", 2), ("ld_l", 3), ("q", 0), ("rg", 1, "v"), ("ld_raw", 6), ("ld_l", 4), ("q", 1), ("rc", 0)]
-    seq += [("mm", 0, 0), ("mm", 0, 1), ("p1", 0, 0), ("rg", 2, "s"), ("rg", 4, "v"), ("ld_raw", 5), ("p1", 0, 1), ("q", 4), ("q", 2), ("ld_raw", 7)]
-    seq += [("mm", 0, 6), ("mm", 0, 7), ("mm", 0, 2), ("mm", 0, 3), ("rg", 3, "s"), ("ld_raw", 8), ("mx", 1), ("ex", 1), ("ld_l", 5), ("mx", 2), ("q", 3), ("mm", 0, 4), ("mm", 0, 5)]
-    seq += [("p1", 0, 2), ("p1", 0, 3), ("mx", 3), ("p1", 0, 4), ("p1", 0, 5), ("p1", 0, 6), ("p1", 0, 7)]
-    seq += [("rg", 6, "s"), ("rg", 5, "s"), ("ld_raw", 9), ("ds", 0), ("c2", 0)]
-    s_extra = {0: [("ex", 2), ("rg", 7, "s")], 1: [("ex", 3), ("rg", 8, "s")], 2: [("ex", 4), ("rg", 9, "s")], 3: [("ex", 5)], 4: [("ex", 6)], 5: [("ex", 7)]}
-    v_extra = {0: [("mx", 4)], 1: [("mx", 5)], 2: [("mx", 6), ("q", 5)], 3: [("mx", 7)]}
-    v_late = {0: [("q", 6)], 1: [("q", 7)], 2: [("q", 8)], 3: [("q", 9)]}
+    seq += [("ld_raw", 0), ("ld_l", 0), ("ld_raw", 1), ("ld_raw", 2), ("ld_raw", 3), ("warm",)]
+    seq += [("rg", 0, "s"), ("ld_raw", 4), ("mx", 0), ("ex", 0), ("q", 0)]
+    seq += [("rg", 1, "v"), ("ld_raw", 6), ("ld_l", 1), ("ld_l", 2), ("ld_l", 3), ("rg", 2, "v"), ("ld_raw", 7), ("q", 1), ("rg", 3, "s"), ("ld_raw", 5), ("rc", 0), ("q", 2)]
+    seq += [("rg", 4, "v"), ("ld_raw", 8), ("ld_l", 4)]
+    seq += [("mm", 0, 0), ("mm", 0, 1), ("mm", 0, 2), ("mm", 0, 3), ("p1", 0, 0), ("p1", 0, 1), ("p1", 0, 2), ("p1", 0, 3)]
+    seq += [("mx", 1), ("rg", 6, "s"), ("ex", 1), ("ld_l", 5), ("q", 4), ("q", 3), ("mx", 2), ("ex", 2)]
+    seq += [("mm", 0, 4), ("mm", 0, 5), ("mm", 0, 6), ("mm", 0, 7)]
+    seq += [("p1", 0, 4), ("p1", 0, 5), ("p1", 0, 6), ("p1", 0, 7)]
+    seq += [("rg", 5, "s"), ("ld_raw", 9), ("q", 6), ("ds", 0), ("rc", 1), ("mx", 3), ("c2", 0), ("u", 0), ("rg", 7, "s")]
+    s_extra = {0: [("ex", 3), ("rg", 8, "s")], 1: [("ex", 4), ("rg", 9, "s")], 2: [("ex", 5)], 3: [("ex", 6)], 4: [("ex", 7)]}
+    v_extra = {0: [("q", 7), ("mx", 4)], 1: [("q", 5), ("q", 8), ("mx", 5)], 2: [("q", 9), ("mx", 6)], 3: [("mx", 7)]}
     l_extra = {0: [("ld_l", 6)], 1: [("ld_l", 7)]}
-    for t in range(NT):
-        seq += [("u", t)]
+    for t in range(NT - 1):
+        seq += [("mm", t + 1, j) for j in range(NB)]
+        seq += [("p1", t + 1, j) for j in range(NB)]
+        seq += [("p2g", t), ("st", t, 2048, 4096)]
+        seq += [("p2v", t, 0), ("ds", t + 1)]
+        seq += [("p2v", t, 1), ("c2", t + 1), ("u", t + 1)]
+        if t + 2 < NT:
+            seq += [("rc", t + 2)]
+        seq += [("p2v", t, 2), ("st", t, 0, 2048)]
         seq += l_extra.get(t, [])
         seq += s_extra.get(t, [])
         seq += v_extra.get(t, [])
-        seq += [("p2v", t), ("st", t, 0)]
-        seq += v_late.get(t, [])
-        if t + 1 < NT:
-            seq += [("rc", t + 1)]
-            seq += [("mm", t + 1, j) for j in range(NB)]
-            seq += [("p1", t + 1, j) for j in range(NB)]
-        seq += [("p2g", t), ("st", t, 1)]
-        if t + 1 < NT:
-            seq += [("ds", t + 1), ("c2", t + 1)]
+    for h in range(4):
+        seq += [("p2v", NT - 1, h), ("st", NT - 1, h * 1024, (h + 1) * 1024)]
     return seq
 
 
@@ -187,14 +190,13 @@ def tile_spatialgather_module_kernel(tc, feats, probs, grad_out, out):
                 out=c2[t][:], in0=dsum[t][:], scalar1=rs[t][:], scalar2=-1.0, op0=ALU.mult, op1=ALU.mult,
             )
 
-        def p2v(t):
-            step = VCOLS[t] if VCOLS[t] < N else CH
-            for c0 in range(0, VCOLS[t], step):
-                cols = slice(c0, c0 + step)
-                nc.vector.scalar_tensor_tensor(
-                    out=tt[t][:, cols], in0=et[t][:, cols], scalar=c2[t][:], in1=tt[t][:, cols],
-                    op0=ALU.mult, op1=ALU.add,
-                )
+        def p2v(t, h):
+            lo, hi = VPIECES[h] if VCOLS[t] < N else (h * CH, (h + 1) * CH)
+            cols = slice(lo, hi)
+            nc.vector.scalar_tensor_tensor(
+                out=tt[t][:, cols], in0=et[t][:, cols], scalar=c2[t][:], in1=tt[t][:, cols],
+                op0=ALU.mult, op1=ALU.add,
+            )
 
         def u(t):
             for c0 in range(VCOLS[t], N, USTEP):
@@ -206,14 +208,9 @@ def tile_spatialgather_module_kernel(tc, feats, probs, grad_out, out):
                 cols = slice(c0, c0 + GSTEP)
                 nc.gpsimd.tensor_tensor(out=tt[t][:, cols], in0=tt[t][:, cols], in1=et[t][:, cols], op=ALU.add)
 
-        def st(t, h):
+        def st(t, lo, hi):
             b, kt = divmod(t, KT)
-            if VCOLS[t] < N:
-                parts = [slice(0, VCOLS[t])] if h == 0 else [slice(VCOLS[t], N)]
-            else:
-                parts = [slice(c0, c0 + CH) for c0 in range(0, N, CH)] if h == 0 else []
-            for cols in parts:
-                nc.sync.dma_start(out=o_v[b, kt][:, cols], in_=tt[t][:, cols])
+            nc.sync.dma_start(out=o_v[b, kt][:, lo:hi], in_=tt[t][:, lo:hi])
 
         ops = {
             "ld_raw": ld_raw, "ld_l": ld_l, "warm": warm, "rg": rg, "q": q, "mx": mx, "ex": ex, "rc": rc,

@@ -1,6 +1,7 @@
 from contextlib import ExitStack
 
 import concourse.mybir as mybir
+from concourse.masks import make_identity
 
 FLOPS = 2 * 2 * 512 * 512 * 4096
 
@@ -27,9 +28,13 @@ BANK = 512
 NB = N // BANK
 GSTEP = 512
 USTEP = 512
-VPIECES = [(0, 768), (768, 1408), (1408, 2048)]
+VPIECES = {2048: [(0, 768), (768, 1408), (1408, 2048)], 1536: [(0, 576), (576, 1088), (1088, 1536)]}
+TCOLS = {4: (1536, 2048), 5: (1536, 2048), 6: (1536, 2048), 7: (0, 1024)}
+LASTV = [(1024, 2048), (2048, 3072), (3072, 4096)]
+NPRE = 6
 ITEMS = [("g", 0, 0), ("x", 0, 0), ("x", 0, 1), ("x", 0, 2), ("x", 0, 3), ("g", 1, 0), ("x", 1, 0), ("x", 1, 1), ("x", 1, 2), ("x", 1, 3)]
-VCOLS = [2048, 2048, 2048, 2048, 2048, 2048, 2048, 4096]
+VCOLS = [2048, 2048, 2048, 2048, 1536, 1536, 1536, 4096]
+GLO = 2048
 
 
 def build_order():
@@ -47,19 +52,37 @@ def build_order():
     v_extra = {0: [("q", 7), ("mx", 4)], 1: [("q", 5), ("q", 8), ("mx", 5)], 2: [("q", 9), ("mx", 6)], 3: [("mx", 7)]}
     l_extra = {0: [("ld_l", 6)], 1: [("ld_l", 7)]}
     for t in range(NT - 1):
-        seq += [("mm", t + 1, j) for j in range(NB)]
-        seq += [("p1", t + 1, j) for j in range(NB)]
-        seq += [("p2g", t), ("st", t, 2048, 4096)]
-        seq += [("p2v", t, 0), ("ds", t + 1)]
-        seq += [("p2v", t, 1), ("c2", t + 1), ("u", t + 1)]
+        n = t + 1
+        if t not in TCOLS:
+            seq += [("mm", n, j) for j in range(NB)]
+        seq += [("p1", n, j) for j in range(NB)]
+        seq += [("p2g", t), ("st", t, GLO, 4096)]
+        pcs = [(c, c + BANK) for c in range(TCOLS[n][0], TCOLS[n][1], BANK)] if n in TCOLS else []
+        if pcs:
+            if n + 1 < NT:
+                seq += [("mm", n + 1, j) for j in range(NPRE)]
+            seq += [("pma", n, c) for c, e in pcs]
+        seq += [("p2v", t, 0), ("ds", n)]
+        seq += [("p2v", t, 1), ("c2", n)]
+        if pcs:
+            seq += [("dg", n)] + [("pmb", n, c) for c, e in pcs]
+        seq += [("u", n)]
+        if pcs:
+            seq += [("pe", n, c) for c, e in pcs]
+            if n + 1 < NT:
+                seq += [("mm", n + 1, j) for j in range(NPRE, NB)]
         if t + 2 < NT:
             seq += [("rc", t + 2)]
-        seq += [("p2v", t, 2), ("st", t, 0, 2048)]
+        seq += [("p2v", t, 2), ("st", t, 0, VCOLS[t])]
+        if pcs and n + 1 < NT:
+            seq += [("st", n, pcs[0][0], pcs[-1][1])]
         seq += l_extra.get(t, [])
         seq += s_extra.get(t, [])
         seq += v_extra.get(t, [])
-    for h in range(4):
-        seq += [("p2v", NT - 1, h), ("st", NT - 1, h * 1024, (h + 1) * 1024)]
+    for h in range(len(LASTV)):
+        if h == len(LASTV) - 1:
+            seq += [("st", NT - 1, TCOLS[NT - 1][0], TCOLS[NT - 1][1])]
+        seq += [("p2v", NT - 1, h), ("st", NT - 1, LASTV[h][0], LASTV[h][1])]
     return seq
 
 
@@ -78,13 +101,19 @@ def tile_spatialgather_module_kernel(tc, feats, probs, grad_out, out):
         epool = ctx.enter_context(tc.tile_pool(name="epool", bufs=3))
         tpool = ctx.enter_context(tc.tile_pool(name="tpool", bufs=3))
         small = ctx.enter_context(tc.tile_pool(name="small", bufs=4))
-        psum = ctx.enter_context(tc.psum_pool(name="psum", bufs=8))
+        psum = ctx.enter_context(tc.psum_pool(name="psum", bufs=6))
+        psadd = ctx.enter_context(tc.psum_pool(name="psadd", bufs=2))
+        dgp = ctx.enter_context(tc.tile_pool(name="dgp", bufs=2))
 
         g_codes = keep.tile([P, B * K], U32, name="g_codes", align_bytes=64)
         g_scales = keep.tile([P, B * K], U8, name="g_scales", align_bytes=64)
         x_codes = [keep.tile([P, N], U32, name="x_codes%d" % b, align_bytes=64) for b in range(B)]
         x_scales = [keep.tile([P, N], U8, name="x_scales%d" % b, align_bytes=64) for b in range(B)]
 
+        ident = keep.tile([P, P], F32, name="ident")
+        make_identity(nc, ident[:])
+        dgt = {}
+        pp = {}
         raw = {}
         grp = {}
         lt = {}
@@ -191,7 +220,7 @@ def tile_spatialgather_module_kernel(tc, feats, probs, grad_out, out):
             )
 
         def p2v(t, h):
-            lo, hi = VPIECES[h] if VCOLS[t] < N else (h * CH, (h + 1) * CH)
+            lo, hi = VPIECES[VCOLS[t]][h] if VCOLS[t] < N else LASTV[h]
             cols = slice(lo, hi)
             nc.vector.scalar_tensor_tensor(
                 out=tt[t][:, cols], in0=et[t][:, cols], scalar=c2[t][:], in1=tt[t][:, cols],
@@ -199,14 +228,28 @@ def tile_spatialgather_module_kernel(tc, feats, probs, grad_out, out):
             )
 
         def u(t):
-            for c0 in range(VCOLS[t], N, USTEP):
+            for c0 in range(GLO if VCOLS[t] < N else N, N, USTEP):
                 cols = slice(c0, c0 + USTEP)
                 nc.scalar.activation(out=et[t][:, cols], in_=et[t][:, cols], func=ACT.Copy, scale=c2[t][:])
 
         def p2g(t):
-            for c0 in range(VCOLS[t], N, GSTEP):
+            for c0 in range(GLO if VCOLS[t] < N else N, N, GSTEP):
                 cols = slice(c0, c0 + GSTEP)
                 nc.gpsimd.tensor_tensor(out=tt[t][:, cols], in0=tt[t][:, cols], in1=et[t][:, cols], op=ALU.add)
+
+        def dgf(t):
+            dgt[t] = dgp.tile([P, P], F32, name="dgt", tag="dgt")
+            nc.scalar.activation(out=dgt[t][:], in_=ident[:], func=ACT.Copy, scale=c2[t][:])
+
+        def pma(t, c0):
+            pp[(t, c0)] = psadd.tile([P, BANK], F32, name="pp", tag="pp")
+            nc.tensor.matmul(out=pp[(t, c0)][:], lhsT=ident[:], rhs=tt[t][:, c0 : c0 + BANK], start=True, stop=False)
+
+        def pmb(t, c0):
+            nc.tensor.matmul(out=pp[(t, c0)][:], lhsT=dgt[t][:], rhs=et[t][:, c0 : c0 + BANK], start=False, stop=True)
+
+        def pe(t, c0):
+            nc.scalar.copy(out=tt[t][:, c0 : c0 + BANK], in_=pp[(t, c0)][:])
 
         def st(t, lo, hi):
             b, kt = divmod(t, KT)
@@ -214,7 +257,7 @@ def tile_spatialgather_module_kernel(tc, feats, probs, grad_out, out):
 
         ops = {
             "ld_raw": ld_raw, "ld_l": ld_l, "warm": warm, "rg": rg, "q": q, "mx": mx, "ex": ex, "rc": rc,
-            "mm": mm, "p1": p1, "ds": ds, "c2": c2f, "p2v": p2v, "u": u, "p2g": p2g, "st": st,
+            "mm": mm, "p1": p1, "ds": ds, "c2": c2f, "p2v": p2v, "u": u, "p2g": p2g, "st": st, "dg": dgf, "pma": pma, "pmb": pmb, "pe": pe,
         }
         with tc.manual_schedule():
             for step in build_order():

@@ -28,13 +28,14 @@ BANK = 512
 NB = N // BANK
 GSTEP = 512
 USTEP = 512
-VPIECES = {2048: [(0, 768), (768, 1408), (1408, 2048)], 1536: [(0, 576), (576, 1088), (1088, 1536)]}
-TCOLS = {4: (1536, 2048), 5: (1536, 2048), 6: (1536, 2048), 7: (0, 1024)}
-LASTV = [(1024, 2048), (2048, 3072), (3072, 4096)]
+VPIECES = {2048: [(0, 768), (768, 1408), (1408, 2048)], 1280: [(0, 480), (480, 880), (880, 1280)]}
+TCOLS = {3: (1280, 2304), 4: (1280, 2304), 5: (1280, 2304), 6: (1280, 2304), 7: (0, 1536)}
+LASTV = [(1536, 2560), (2560, 3456), (3456, 4096)]
 NPRE = 6
 ITEMS = [("g", 0, 0), ("x", 0, 0), ("x", 0, 1), ("x", 0, 2), ("x", 0, 3), ("g", 1, 0), ("x", 1, 0), ("x", 1, 1), ("x", 1, 2), ("x", 1, 3)]
-VCOLS = [2048, 2048, 2048, 2048, 1536, 1536, 1536, 4096]
-GLO = 2048
+VCOLS = [2048, 2048, 2048, 1280, 1280, 1280, 1280, 4096]
+GLO = [2048, 2048, 2048, 2304, 2304, 2304, 2304, 4096]
+NGP = 4
 
 
 def build_order():
@@ -56,7 +57,7 @@ def build_order():
         if t not in TCOLS:
             seq += [("mm", n, j) for j in range(NB)]
         seq += [("p1", n, j) for j in range(NB)]
-        seq += [("p2g", t), ("st", t, GLO, 4096)]
+        seq += [("p2g", t), ("st", t, GLO[t], 4096)]
         pcs = [(c, c + BANK) for c in range(TCOLS[n][0], TCOLS[n][1], BANK)] if n in TCOLS else []
         if pcs:
             if n + 1 < NT:
@@ -69,8 +70,6 @@ def build_order():
         seq += [("u", n)]
         if pcs:
             seq += [("pe", n, c) for c, e in pcs]
-            if n + 1 < NT:
-                seq += [("mm", n + 1, j) for j in range(NPRE, NB)]
         if t + 2 < NT:
             seq += [("rc", t + 2)]
         seq += [("p2v", t, 2), ("st", t, 0, VCOLS[t])]
@@ -79,6 +78,8 @@ def build_order():
         seq += l_extra.get(t, [])
         seq += s_extra.get(t, [])
         seq += v_extra.get(t, [])
+        if pcs and n + 1 < NT:
+            seq += [("mm", n + 1, j) for j in range(NPRE, NB)]
     for h in range(len(LASTV)):
         if h == len(LASTV) - 1:
             seq += [("st", NT - 1, TCOLS[NT - 1][0], TCOLS[NT - 1][1])]
@@ -228,13 +229,13 @@ def tile_spatialgather_module_kernel(tc, feats, probs, grad_out, out):
             )
 
         def u(t):
-            for c0 in range(GLO if VCOLS[t] < N else N, N, USTEP):
-                cols = slice(c0, c0 + USTEP)
+            for c0 in range(GLO[t], N, (N - GLO[t]) // NGP if GLO[t] < N else 1):
+                cols = slice(c0, c0 + (N - GLO[t]) // NGP)
                 nc.scalar.activation(out=et[t][:, cols], in_=et[t][:, cols], func=ACT.Copy, scale=c2[t][:])
 
         def p2g(t):
-            for c0 in range(GLO if VCOLS[t] < N else N, N, GSTEP):
-                cols = slice(c0, c0 + GSTEP)
+            for c0 in range(GLO[t], N, (N - GLO[t]) // NGP if GLO[t] < N else 1):
+                cols = slice(c0, c0 + (N - GLO[t]) // NGP)
                 nc.gpsimd.tensor_tensor(out=tt[t][:, cols], in0=tt[t][:, cols], in1=et[t][:, cols], op=ALU.add)
 
         def dgf(t):
@@ -242,7 +243,10 @@ def tile_spatialgather_module_kernel(tc, feats, probs, grad_out, out):
             nc.scalar.activation(out=dgt[t][:], in_=ident[:], func=ACT.Copy, scale=c2[t][:])
 
         def pma(t, c0):
-            pp[(t, c0)] = psadd.tile([P, BANK], F32, name="pp", tag="pp")
+            if t == NT - 1:
+                pp[(t, c0)] = psum.tile([P, BANK], F32, name="ps", tag="ps")
+            else:
+                pp[(t, c0)] = psadd.tile([P, BANK], F32, name="pp", tag="pp")
             nc.tensor.matmul(out=pp[(t, c0)][:], lhsT=ident[:], rhs=tt[t][:, c0 : c0 + BANK], start=True, stop=False)
 
         def pmb(t, c0):

@@ -13,7 +13,6 @@ E4X4 = mybir.dt.float8_e4m3fn_x4
 E5X4 = mybir.dt.float8_e5m2_x4
 ALU = mybir.AluOpType
 ACT = mybir.ActivationFunctionType
-AXIS = mybir.AxisListType
 
 P = 128
 PACK = 4
@@ -29,13 +28,13 @@ NB = N // BANK
 GSTEP = 512
 USTEP = 512
 VPIECES = {2048: [(0, 768), (768, 1408), (1408, 2048)], 1280: [(0, 480), (480, 880), (880, 1280)]}
-TCOLS = {3: (1280, 2304), 4: (1280, 2304), 5: (1280, 2304), 6: (1280, 2304), 7: (0, 1536)}
-LASTV = [(1536, 2560), (2560, 3456), (3456, 4096)]
+TCOLS = {3: (1280, 2304), 4: (1280, 2304), 5: (1280, 2304), 6: (1280, 2304), 7: (0, 1024)}
+LASTV = [(1024, 1536), (1536, 2304), (2304, 3200), (3200, 4096)]
 NPRE = 6
 ITEMS = [("g", 0, 0), ("x", 0, 0), ("x", 0, 1), ("x", 0, 2), ("x", 0, 3), ("g", 1, 0), ("x", 1, 0), ("x", 1, 1), ("x", 1, 2), ("x", 1, 3)]
 VCOLS = [2048, 2048, 2048, 1280, 1280, 1280, 1280, 4096]
 GLO = [2048, 2048, 2048, 2304, 2304, 2304, 2304, 4096]
-NGP = 4
+NGP = [4] * 7 + [1]
 
 
 def build_order():
@@ -48,42 +47,46 @@ def build_order():
     seq += [("mx", 1), ("rg", 6, "s"), ("ex", 1), ("ld_l", 5), ("q", 4), ("q", 3), ("mx", 2), ("ex", 2)]
     seq += [("mm", 0, 4), ("mm", 0, 5), ("mm", 0, 6), ("mm", 0, 7)]
     seq += [("p1", 0, 4), ("p1", 0, 5), ("p1", 0, 6), ("p1", 0, 7)]
-    seq += [("rg", 5, "s"), ("ld_raw", 9), ("q", 6), ("ds", 0), ("rc", 1), ("mx", 3), ("c2", 0), ("u", 0), ("rg", 7, "s")]
-    s_extra = {0: [("ex", 3), ("rg", 8, "s")], 1: [("ex", 4), ("rg", 9, "s")], 2: [("ex", 5)], 3: [("ex", 6)], 4: [("ex", 7)]}
-    v_extra = {0: [("q", 7), ("mx", 4)], 1: [("q", 5), ("q", 8), ("mx", 5)], 2: [("q", 9), ("mx", 6)], 3: [("mx", 7)]}
+    seq += [("ld_raw", 9), ("q", 6), ("rc", 1), ("c2", 0), ("mx", 3), ("u", 0), ("rg", 7, "s"), ("rg", 8, "s")]
+    s_extra = {0: [("ex", 3), ("rg", 5, "s")], 1: [("rg", 9, "s"), ("ex", 4)], 2: [("ex", 5)], 3: [("ex", 6)], 4: [("ex", 7)]}
+    q_extra = {0: [("q", 7)], 1: [("q", 8)], 2: [("q", 5), ("q", 9)]}
+    v_extra = {0: [("mx", 4)], 1: [("mx", 5)], 2: [("mx", 6)], 3: [("mx", 7)]}
     l_extra = {0: [("ld_l", 6)], 1: [("ld_l", 7)]}
     for t in range(NT - 1):
         n = t + 1
         if t not in TCOLS:
             seq += [("mm", n, j) for j in range(NB)]
+        if n > 1:
+            seq += [("rc", n)]
         seq += [("p1", n, j) for j in range(NB)]
-        seq += [("p2g", t), ("st", t, GLO[t], 4096)]
+        seq += [("p2g", t)]
+        if t < 6:
+            seq += [("st", t, GLO[t], 4096)]
+        if t in TCOLS:
+            seq += [("st", t, TCOLS[t][0], TCOLS[t][1])]
         pcs = [(c, c + BANK) for c in range(TCOLS[n][0], TCOLS[n][1], BANK)] if n in TCOLS else []
         if pcs:
-            if n + 1 < NT:
+            if n + 1 < NT and n != KT - 1:
                 seq += [("mm", n + 1, j) for j in range(NPRE)]
             seq += [("pma", n, c) for c, e in pcs]
-        seq += [("p2v", t, 0), ("ds", n)]
-        seq += [("p2v", t, 1), ("c2", n)]
+        if t < NT - 2:
+            seq += [("p2v", t, 0), ("p2v", t, 1), ("p2v", t, 2), ("st", t, 0, VCOLS[t])] + q_extra.get(t, [])
+        seq += [("c2", n)]
+        if n == NT - 2:
+            seq += [("p2v", n, 0), ("p2v", n, 1), ("p2v", n, 2), ("st", n, 0, VCOLS[n])]
         if pcs:
+            if n + 1 < NT:
+                seq += [("mm", n + 1, j) for j in range(NPRE if n != KT - 1 else 0, NB)]
             seq += [("dg", n)] + [("pmb", n, c) for c, e in pcs]
-        seq += [("u", n)]
+        seq += [("u", n)] + s_extra.get(t, [])
         if pcs:
             seq += [("pe", n, c) for c, e in pcs]
-        if t + 2 < NT:
-            seq += [("rc", t + 2)]
-        seq += [("p2v", t, 2), ("st", t, 0, VCOLS[t])]
-        if pcs and n + 1 < NT:
-            seq += [("st", n, pcs[0][0], pcs[-1][1])]
         seq += l_extra.get(t, [])
-        seq += s_extra.get(t, [])
         seq += v_extra.get(t, [])
-        if pcs and n + 1 < NT:
-            seq += [("mm", n + 1, j) for j in range(NPRE, NB)]
     for h in range(len(LASTV)):
-        if h == len(LASTV) - 1:
-            seq += [("st", NT - 1, TCOLS[NT - 1][0], TCOLS[NT - 1][1])]
         seq += [("p2v", NT - 1, h), ("st", NT - 1, LASTV[h][0], LASTV[h][1])]
+        if 0 < h < 3:
+            seq += [("st", NT - 1, (h - 1) * BANK, h * BANK)]
     return seq
 
 
@@ -125,7 +128,6 @@ def tile_spatialgather_module_kernel(tc, feats, probs, grad_out, out):
         ssum = {}
         rs = {}
         dparts = {}
-        dsum = {}
         c2 = {}
 
         def ld_raw(i):
@@ -210,14 +212,11 @@ def tile_spatialgather_module_kernel(tc, feats, probs, grad_out, out):
                 op0=ALU.mult, op1=ALU.mult, accum_out=dparts[t][:, j : j + 1],
             )
 
-        def ds(t):
-            dsum[t] = small.tile([P, 1], F32, name="dsum", tag="dsum")
-            nc.vector.tensor_reduce(out=dsum[t][:], in_=dparts[t][:], axis=AXIS.X, op=ALU.add)
-
         def c2f(t):
             c2[t] = small.tile([P, 1], F32, name="c2", tag="c2")
             nc.vector.tensor_scalar(
-                out=c2[t][:], in0=dsum[t][:], scalar1=rs[t][:], scalar2=-1.0, op0=ALU.mult, op1=ALU.mult,
+                out=dparts[t][:], in0=dparts[t][:], scalar1=rs[t][:], scalar2=None,
+                op0=ALU.mult, op1=ALU.subtract, accum_out=c2[t][:],
             )
 
         def p2v(t, h):
@@ -229,14 +228,16 @@ def tile_spatialgather_module_kernel(tc, feats, probs, grad_out, out):
             )
 
         def u(t):
-            for c0 in range(GLO[t], N, (N - GLO[t]) // NGP if GLO[t] < N else 1):
-                cols = slice(c0, c0 + (N - GLO[t]) // NGP)
+            for c0 in range(GLO[t], N, max((N - GLO[t]) // NGP[t], 1)):
+                cols = slice(c0, c0 + (N - GLO[t]) // NGP[t])
                 nc.scalar.activation(out=et[t][:, cols], in_=et[t][:, cols], func=ACT.Copy, scale=c2[t][:])
 
         def p2g(t):
-            for c0 in range(GLO[t], N, (N - GLO[t]) // NGP if GLO[t] < N else 1):
-                cols = slice(c0, c0 + (N - GLO[t]) // NGP)
+            for c0 in range(GLO[t], N, max((N - GLO[t]) // NGP[t], 1)):
+                cols = slice(c0, c0 + (N - GLO[t]) // NGP[t])
                 nc.gpsimd.tensor_tensor(out=tt[t][:, cols], in0=tt[t][:, cols], in1=et[t][:, cols], op=ALU.add)
+                if t >= 6:
+                    st(t, cols.start, cols.stop)
 
         def dgf(t):
             dgt[t] = dgp.tile([P, P], F32, name="dgt", tag="dgt")
@@ -261,7 +262,7 @@ def tile_spatialgather_module_kernel(tc, feats, probs, grad_out, out):
 
         ops = {
             "ld_raw": ld_raw, "ld_l": ld_l, "warm": warm, "rg": rg, "q": q, "mx": mx, "ex": ex, "rc": rc,
-            "mm": mm, "p1": p1, "ds": ds, "c2": c2f, "p2v": p2v, "u": u, "p2g": p2g, "st": st, "dg": dgf, "pma": pma, "pmb": pmb, "pe": pe,
+            "mm": mm, "p1": p1, "c2": c2f, "p2v": p2v, "u": u, "p2g": p2g, "st": st, "dg": dgf, "pma": pma, "pmb": pmb, "pe": pe,
         }
         with tc.manual_schedule():
             for step in build_order():

@@ -30,6 +30,7 @@ USTEP = 512
 VPIECES = {2048: [(0, 768), (768, 1408), (1408, 2048)], 1280: [(0, 480), (480, 880), (880, 1280)]}
 TCOLS = {3: (1280, 2304), 4: (1280, 2304), 5: (1280, 2304), 6: (1280, 2304), 7: (0, 1024)}
 LASTV = [(1024, 1536), (1536, 2304), (2304, 3200), (3200, 4096)]
+LSPLIT = {0: 2}
 NPRE = 6
 ITEMS = [("g", 0, 0), ("x", 0, 0), ("x", 0, 1), ("x", 0, 2), ("x", 0, 3), ("g", 1, 0), ("x", 1, 0), ("x", 1, 1), ("x", 1, 2), ("x", 1, 3)]
 VCOLS = [2048, 2048, 2048, 1280, 1280, 1280, 1280, 4096]
@@ -39,25 +40,23 @@ NGP = [4] * 7 + [1]
 
 def build_order():
     seq = []
-    seq += [("ld_raw", 0), ("ld_l", 0), ("ld_raw", 1), ("ld_raw", 2), ("ld_raw", 3), ("warm",)]
-    seq += [("rg", 0, "s"), ("ld_raw", 4), ("mx", 0), ("ex", 0), ("q", 0)]
-    seq += [("rg", 1, "v"), ("ld_raw", 6), ("ld_l", 1), ("ld_l", 2), ("ld_l", 3), ("rg", 2, "v"), ("ld_raw", 7), ("q", 1), ("rg", 3, "s"), ("ld_raw", 5), ("rc", 0), ("q", 2)]
-    seq += [("rg", 4, "v"), ("ld_raw", 8), ("ld_l", 4)]
-    seq += [("mm", 0, 0), ("mm", 0, 1), ("mm", 0, 2), ("mm", 0, 3), ("p1", 0, 0), ("p1", 0, 1), ("p1", 0, 2), ("p1", 0, 3)]
-    seq += [("mx", 1), ("rg", 6, "s"), ("ex", 1), ("ld_l", 5), ("q", 4), ("q", 3), ("mx", 2), ("ex", 2)]
-    seq += [("mm", 0, 4), ("mm", 0, 5), ("mm", 0, 6), ("mm", 0, 7)]
-    seq += [("p1", 0, 4), ("p1", 0, 5), ("p1", 0, 6), ("p1", 0, 7)]
-    seq += [("ld_raw", 9), ("q", 6), ("rc", 1), ("c2", 0), ("mx", 3), ("u", 0), ("rg", 7, "s"), ("rg", 8, "s")]
-    s_extra = {0: [("ex", 3), ("rg", 5, "s")], 1: [("rg", 9, "s"), ("ex", 4)], 2: [("ex", 5)], 3: [("ex", 6)], 4: [("ex", 7)]}
-    q_extra = {0: [("q", 7)], 1: [("q", 8)], 2: [("q", 5), ("q", 9)]}
+    seq += [("ld_l", 0), ("ld_raw", 0), ("ld_l", 1), ("ld_raw", 1), ("ld_raw", 2), ("warm",)]
+    seq += [("mx", 0), ("ex", 0), ("rg", 0, "v"), ("ld_raw", 3), ("ld_raw", 4), ("mx", 1), ("ex", 1), ("q", 0)]
+    seq += [("rg", 1, "v"), ("ld_l", 2), ("ld_raw", 6), ("rg", 2, "v"), ("ld_l", 3), ("ld_raw", 7), ("q", 1), ("rg", 3, "s"), ("rg", 4, "s"), ("rc", 0), ("q", 2)]
+    seq += [("mm", 0, 0), ("mm", 0, 1), ("mm", 0, 2), ("mm", 0, 3)]
+    seq += [("p1", 0, 0), ("p1", 0, 1), ("p1", 0, 2), ("p1", 0, 3), ("mx", 2), ("ex", 2), ("ld_raw", 8), ("ld_l", 4)]
+    seq += [("q", 3), ("mm", 0, 4), ("mm", 0, 5), ("rc", 1), ("p1", 0, 4), ("p1", 0, 5), ("q", 4), ("ld_raw", 5), ("ld_l", 5)]
+    seq += [("mm", 0, 6), ("mm", 0, 7)]
+    seq += [("p1", 0, 6), ("p1", 0, 7)]
+    seq += [("ld_raw", 9), ("c2", 0), ("mx", 3), ("u", 0), ("rg", 6, "s"), ("rg", 7, "s")]
+    s_extra = {0: [("ex", 3), ("rg", 8, "s"), ("rg", 5, "s")], 1: [("rg", 9, "s"), ("ex", 4)], 2: [("ex", 5)], 3: [("ex", 6)], 4: [("ex", 7)]}
+    q_extra = {0: [("q", 6)], 1: [("q", 7), ("q", 8)], 2: [("q", 5), ("q", 9)]}
     v_extra = {0: [("mx", 4)], 1: [("mx", 5)], 2: [("mx", 6)], 3: [("mx", 7)]}
     l_extra = {0: [("ld_l", 6)], 1: [("ld_l", 7)]}
     for t in range(NT - 1):
         n = t + 1
         if t not in TCOLS:
             seq += [("mm", n, j) for j in range(NB)]
-        if n > 1:
-            seq += [("rc", n)]
         seq += [("p1", n, j) for j in range(NB)]
         seq += [("p2g", t)]
         if t < 6:
@@ -70,10 +69,14 @@ def build_order():
                 seq += [("mm", n + 1, j) for j in range(NPRE)]
             seq += [("pma", n, c) for c, e in pcs]
         if t < NT - 2:
-            seq += [("p2v", t, 0), ("p2v", t, 1), ("p2v", t, 2), ("st", t, 0, VCOLS[t])] + q_extra.get(t, [])
+            seq += [("p2v", t, 0), ("st", t, 0, VCOLS[t])] + q_extra.get(t, [])
+        if t not in v_extra and n + 1 < NT:
+            seq += [("rc", n + 1)]
         seq += [("c2", n)]
+        if t in v_extra:
+            seq += [("rc", n + 1)] + v_extra[t]
         if n == NT - 2:
-            seq += [("p2v", n, 0), ("p2v", n, 1), ("p2v", n, 2), ("st", n, 0, VCOLS[n])]
+            seq += [("p2v", n, 0), ("st", n, 0, VCOLS[n])]
         if pcs:
             if n + 1 < NT:
                 seq += [("mm", n + 1, j) for j in range(NPRE if n != KT - 1 else 0, NB)]
@@ -82,7 +85,6 @@ def build_order():
         if pcs:
             seq += [("pe", n, c) for c, e in pcs]
         seq += l_extra.get(t, [])
-        seq += v_extra.get(t, [])
     for h in range(len(LASTV)):
         seq += [("p2v", NT - 1, h), ("st", NT - 1, LASTV[h][0], LASTV[h][1])]
         if 0 < h < 3:
@@ -142,7 +144,9 @@ def tile_spatialgather_module_kernel(tc, feats, probs, grad_out, out):
         def ld_l(t):
             b, kt = divmod(t, KT)
             lt[t] = lpool.tile([P, N], BF16, name="lt", tag="lt")
-            nc.sync.dma_start(out=lt[t][:], in_=l_v[b, kt])
+            for lo in range(0, N, N // LSPLIT.get(t, 1)):
+                hi = lo + N // LSPLIT.get(t, 1)
+                nc.sync.dma_start(out=lt[t][:, lo:hi], in_=l_v[b, kt][:, lo:hi])
 
         def warm():
             w0 = small.tile([P, 1], F32, name="w0", tag="w0")
@@ -170,11 +174,15 @@ def tile_spatialgather_module_kernel(tc, feats, probs, grad_out, out):
             nc.vector.quantize_mx(out=codes, scales=scales, in_=grp[i][:].rearrange("p w j -> p (w j)"))
 
         def mx(t):
-            negm[t] = small.tile([P, 1], F32, name="negm", tag="negm")
-            nc.vector.tensor_scalar(
-                out=lt[t][:], in0=lt[t][:], scalar1=-1.0, scalar2=None,
-                op0=ALU.mult, op1=ALU.min, accum_out=negm[t][:],
-            )
+            start = None
+            for lo in range(0, N, N // LSPLIT.get(t, 1)):
+                hi = lo + N // LSPLIT.get(t, 1)
+                negm[t] = small.tile([P, 1], F32, name="negm", tag="negm")
+                nc.vector.tensor_scalar(
+                    out=lt[t][:, lo:hi], in0=lt[t][:, lo:hi], scalar1=-1.0, scalar2=start,
+                    op0=ALU.mult, op1=ALU.min, accum_out=negm[t][:],
+                )
+                start = negm[t][:]
 
         def ex(t):
             et[t] = epool.tile([P, N], F32, name="et", tag="et")
@@ -220,7 +228,7 @@ def tile_spatialgather_module_kernel(tc, feats, probs, grad_out, out):
             )
 
         def p2v(t, h):
-            lo, hi = VPIECES[VCOLS[t]][h] if VCOLS[t] < N else LASTV[h]
+            lo, hi = (0, VCOLS[t]) if VCOLS[t] < N else LASTV[h]
             cols = slice(lo, hi)
             nc.vector.scalar_tensor_tensor(
                 out=tt[t][:, cols], in0=et[t][:, cols], scalar=c2[t][:], in1=tt[t][:, cols],

@@ -44,13 +44,13 @@ def build_order():
     seq += [("mx", 0), ("ex", 0), ("rg", 0, "v"), ("ld_raw", 3), ("ld_raw", 4), ("mx", 1), ("ex", 1), ("q", 0)]
     seq += [("rg", 1, "v"), ("ld_l", 2), ("ld_raw", 6), ("rg", 2, "v"), ("ld_l", 3), ("ld_raw", 7), ("q", 1), ("rg", 3, "s"), ("rg", 4, "s"), ("rc", 0), ("q", 2)]
     seq += [("mm", 0, 0), ("mm", 0, 1), ("mm", 0, 2), ("mm", 0, 3)]
-    seq += [("p1", 0, 0), ("p1", 0, 1), ("p1", 0, 2), ("p1", 0, 3), ("mx", 2), ("ex", 2), ("ld_raw", 8), ("ld_l", 4)]
-    seq += [("q", 3), ("mm", 0, 4), ("mm", 0, 5), ("rc", 1), ("p1", 0, 4), ("p1", 0, 5), ("q", 4), ("ld_raw", 5), ("ld_l", 5)]
+    seq += [("p1", 0, 0), ("p1", 0, 1), ("p1", 0, 2), ("p1", 0, 3), ("q", 3), ("mm", 0, 4), ("mm", 0, 5)]
+    seq += [("mx", 2), ("ex", 2), ("ld_raw", 8), ("ld_l", 4), ("rc", 1), ("p1", 0, 4), ("p1", 0, 5), ("q", 4), ("ld_raw", 5), ("ld_l", 5)]
     seq += [("mm", 0, 6), ("mm", 0, 7)]
     seq += [("p1", 0, 6), ("p1", 0, 7)]
     seq += [("ld_raw", 9), ("c2", 0), ("mx", 3), ("u", 0), ("rg", 6, "s"), ("rg", 7, "s")]
-    s_extra = {0: [("ex", 3), ("rg", 8, "s"), ("rg", 5, "s")], 1: [("rg", 9, "s"), ("ex", 4)], 2: [("ex", 5)], 3: [("ex", 6)], 4: [("ex", 7)]}
-    q_extra = {0: [("q", 6)], 1: [("q", 7), ("q", 8)], 2: [("q", 5), ("q", 9)]}
+    s_extra = {0: [("ex", 3), ("rg", 8, "s")], 1: [("rg", 9, "s"), ("ex", 4)], 2: [("ex", 5)], 3: [("ex", 6)], 4: [("ex", 7)]}
+    q_extra = {0: [("q", 6), ("rg", 5, "v")], 1: [("q", 7), ("q", 5)], 2: [("q", 8), ("q", 9)]}
     v_extra = {0: [("mx", 4)], 1: [("mx", 5)], 2: [("mx", 6)], 3: [("mx", 7)]}
     l_extra = {0: [("ld_l", 6)], 1: [("ld_l", 7)]}
     for t in range(NT - 1):

@@ -28,23 +28,23 @@ NB = N // BANK
 GSTEP = 512
 USTEP = 512
 VPIECES = {2048: [(0, 768), (768, 1408), (1408, 2048)], 1280: [(0, 480), (480, 880), (880, 1280)]}
-TCOLS = {3: (1280, 2304), 4: (1280, 2304), 5: (1280, 2304), 6: (1280, 2304), 7: (0, 1024)}
+TCOLS = {3: (1024, 2048), 4: (1024, 2048), 5: (1280, 2304), 6: (1280, 2304), 7: (0, 1024)}
 LASTV = [(1024, 1536), (1536, 2304), (2304, 3200), (3200, 4096)]
 LSPLIT = {0: 2}
 NPRE = 6
-ITEMS = [("g", 0, 0), ("x", 0, 0), ("x", 0, 1), ("x", 0, 2), ("x", 0, 3), ("g", 1, 0), ("x", 1, 0), ("x", 1, 1), ("x", 1, 2), ("x", 1, 3)]
-VCOLS = [2048, 2048, 2048, 1280, 1280, 1280, 1280, 4096]
-GLO = [2048, 2048, 2048, 2304, 2304, 2304, 2304, 4096]
+ITEMS = [("g", 0, 0, 128), ("x", 0, 0), ("x", 0, 1), ("x", 0, 2), ("x", 0, 3), ("g", 1, 0, 512), ("x", 1, 0), ("x", 1, 1), ("x", 1, 2), ("x", 1, 3), ("g", 0, 128, 512)]
+VCOLS = [2048, 2048, 2048, 1024, 1024, 1280, 1280, 4096]
+GLO = [2048, 2048, 2048, 2048, 2048, 2304, 2304, 4096]
 NGP = [4] * 7 + [1]
 
 
 def build_order():
     seq = []
     seq += [("ld_l", 0), ("ld_raw", 0), ("ld_l", 1), ("ld_raw", 1), ("ld_raw", 2), ("warm",)]
-    seq += [("mx", 0), ("ex", 0), ("rg", 0, "v"), ("ld_raw", 3), ("ld_raw", 4), ("mx", 1), ("ex", 1), ("q", 0)]
+    seq += [("mx", 0), ("ex", 0), ("rg", 0, "v"), ("ld_raw", 3), ("ld_raw", 4), ("ld_raw", 10), ("q", 0), ("mx", 1), ("ex", 1)]
     seq += [("rg", 1, "v"), ("ld_l", 2), ("ld_raw", 6), ("rg", 2, "v"), ("ld_l", 3), ("ld_raw", 7), ("q", 1), ("rg", 3, "s"), ("rg", 4, "s"), ("rc", 0), ("q", 2)]
     seq += [("mm", 0, 0), ("mm", 0, 1), ("mm", 0, 2), ("mm", 0, 3)]
-    seq += [("p1", 0, 0), ("p1", 0, 1), ("p1", 0, 2), ("p1", 0, 3), ("q", 3), ("mm", 0, 4), ("mm", 0, 5)]
+    seq += [("p1", 0, 0), ("p1", 0, 1), ("p1", 0, 2), ("p1", 0, 3), ("rg", 10, "v"), ("q", 3), ("mm", 0, 4), ("mm", 0, 5), ("q", 10)]
     seq += [("mx", 2), ("ex", 2), ("ld_raw", 8), ("ld_l", 4), ("rc", 1), ("p1", 0, 4), ("p1", 0, 5), ("q", 4), ("ld_raw", 5), ("ld_l", 5)]
     seq += [("mm", 0, 6), ("mm", 0, 7)]
     seq += [("p1", 0, 6), ("p1", 0, 7)]
@@ -133,11 +133,12 @@ def tile_spatialgather_module_kernel(tc, feats, probs, grad_out, out):
         c2 = {}
 
         def ld_raw(i):
-            kind, b, c = ITEMS[i]
-            if kind == "g":
-                raw[i] = rawp.tile([P, PACK, K], BF16, name="raw", tag="raw")
-                nc.sync.dma_start(out=raw[i][:], in_=g_v[:, b])
+            if ITEMS[i][0] == "g":
+                kind, b, lo, hi = ITEMS[i]
+                raw[i] = rawp.tile([P, PACK, hi - lo], BF16, name="raw", tag="raw")
+                nc.sync.dma_start(out=raw[i][:], in_=g_v[:, b, :, lo:hi])
             else:
+                kind, b, c = ITEMS[i]
                 raw[i] = rawp.tile([P, PACK, CH], BF16, name="raw", tag="raw")
                 nc.sync.dma_start(out=raw[i][:], in_=x_v[b, :, :, c * CH : (c + 1) * CH])
 
@@ -156,7 +157,7 @@ def tile_spatialgather_module_kernel(tc, feats, probs, grad_out, out):
 
         def rg(i, eng):
             copy = nc.vector.tensor_copy if eng == "v" else nc.scalar.copy
-            width = K if ITEMS[i][0] == "g" else CH
+            width = ITEMS[i][3] - ITEMS[i][2] if ITEMS[i][0] == "g" else CH
             grp[i] = grpp.tile([P, width, PACK], BF16, name="grp", tag="grp", align_bytes=64)
             copy(
                 out=grp[i][:].rearrange("p (c i) t -> p c t i", i=4),
@@ -164,14 +165,22 @@ def tile_spatialgather_module_kernel(tc, feats, probs, grad_out, out):
             )
 
         def q(i):
+            if ITEMS[i][0] == "g":
+                kind, b, lo, hi = ITEMS[i]
+                for a in [lo] if lo == 0 else [lo, 2 * lo]:
+                    e = min(2 * a, hi) if lo else hi
+                    nc.vector.quantize_mx(
+                        out=g_codes[:, b * K + a : b * K + e].bitcast(E5X4),
+                        scales=g_scales[:, b * K + a : b * K + e],
+                        in_=grp[i][:, a - lo : e - lo].rearrange("p w j -> p (w j)"),
+                    )
+                return
             kind, b, c = ITEMS[i]
-            if kind == "g":
-                codes = g_codes[:, b * K : (b + 1) * K].bitcast(E5X4)
-                scales = g_scales[:, b * K : (b + 1) * K]
-            else:
-                codes = x_codes[b][:, c * CH : (c + 1) * CH].bitcast(E4X4)
-                scales = x_scales[b][:, c * CH : (c + 1) * CH]
-            nc.vector.quantize_mx(out=codes, scales=scales, in_=grp[i][:].rearrange("p w j -> p (w j)"))
+            nc.vector.quantize_mx(
+                out=x_codes[b][:, c * CH : (c + 1) * CH].bitcast(E4X4),
+                scales=x_scales[b][:, c * CH : (c + 1) * CH],
+                in_=grp[i][:].rearrange("p w j -> p (w j)"),
+            )
 
         def mx(t):
             start = None

@@ -28,13 +28,13 @@ NB = N // BANK
 GSTEP = 512
 USTEP = 512
 VPIECES = {2048: [(0, 768), (768, 1408), (1408, 2048)], 1280: [(0, 480), (480, 880), (880, 1280)]}
-TCOLS = {3: (1024, 2048), 4: (1024, 2048), 5: (1280, 2304), 6: (1280, 2304), 7: (0, 1024)}
+TCOLS = {3: (1280, 2304), 4: (1280, 2304), 5: (1280, 2304), 6: (1280, 2304), 7: (0, 1024)}
 LASTV = [(1024, 1536), (1536, 2304), (2304, 3200), (3200, 4096)]
 LSPLIT = {0: 2}
 NPRE = 6
 ITEMS = [("g", 0, 0, 128), ("x", 0, 0), ("x", 0, 1), ("x", 0, 2), ("x", 0, 3), ("g", 1, 0, 512), ("x", 1, 0), ("x", 1, 1), ("x", 1, 2), ("x", 1, 3), ("g", 0, 128, 512)]
-VCOLS = [2048, 2048, 2048, 1024, 1024, 1280, 1280, 4096]
-GLO = [2048, 2048, 2048, 2048, 2048, 2304, 2304, 4096]
+VCOLS = [2048, 2048, 2048, 1280, 1280, 1280, 1280, 4096]
+GLO = [2048, 2048, 2048, 2304, 2304, 2304, 2304, 4096]
 NGP = [4] * 7 + [1]
 
 
@@ -44,13 +44,13 @@ def build_order():
     seq += [("mx", 0), ("ex", 0), ("rg", 0, "v"), ("ld_raw", 3), ("ld_raw", 4), ("ld_raw", 10), ("q", 0), ("mx", 1), ("ex", 1)]
     seq += [("rg", 1, "v"), ("ld_l", 2), ("ld_raw", 6), ("rg", 2, "v"), ("ld_l", 3), ("ld_raw", 7), ("q", 1), ("rg", 3, "s"), ("rg", 4, "s"), ("rc", 0), ("q", 2)]
     seq += [("mm", 0, 0), ("mm", 0, 1), ("mm", 0, 2), ("mm", 0, 3)]
-    seq += [("p1", 0, 0), ("p1", 0, 1), ("p1", 0, 2), ("p1", 0, 3), ("rg", 10, "v"), ("q", 3), ("mm", 0, 4), ("mm", 0, 5), ("q", 10)]
-    seq += [("mx", 2), ("ex", 2), ("ld_raw", 8), ("ld_l", 4), ("rc", 1), ("p1", 0, 4), ("p1", 0, 5), ("q", 4), ("ld_raw", 5), ("ld_l", 5)]
+    seq += [("p1", 0, 0), ("p1", 0, 1), ("p1", 0, 2), ("p1", 0, 3), ("rg", 10, "v"), ("rgg", 6), ("q", 3), ("mm", 0, 4), ("mm", 0, 5), ("q", 10)]
+    seq += [("mx", 2), ("ex", 2), ("ld_raw", 8), ("ld_l", 4), ("p1", 0, 4), ("q", 4), ("p1", 0, 5), ("rc", 1), ("ld_raw", 5), ("ld_l", 5)]
     seq += [("mm", 0, 6), ("mm", 0, 7)]
     seq += [("p1", 0, 6), ("p1", 0, 7)]
-    seq += [("ld_raw", 9), ("c2", 0), ("mx", 3), ("u", 0), ("rg", 6, "s"), ("rg", 7, "s")]
+    seq += [("ld_raw", 9), ("c2", 0), ("mx", 3), ("u", 0), ("rg", 7, "s"), ("rg", 5, "s")]
     s_extra = {0: [("ex", 3), ("rg", 8, "s")], 1: [("rg", 9, "s"), ("ex", 4)], 2: [("ex", 5)], 3: [("ex", 6)], 4: [("ex", 7)]}
-    q_extra = {0: [("q", 6), ("rg", 5, "v")], 1: [("q", 7), ("q", 5)], 2: [("q", 8), ("q", 9)]}
+    q_extra = {0: [("q", 6)], 1: [("q", 7), ("q", 5)], 2: [("q", 8), ("q", 9)]}
     v_extra = {0: [("mx", 4)], 1: [("mx", 5)], 2: [("mx", 6)], 3: [("mx", 7)]}
     l_extra = {0: [("ld_l", 6)], 1: [("ld_l", 7)]}
     for t in range(NT - 1):
@@ -101,9 +101,9 @@ def tile_spatialgather_module_kernel(tc, feats, probs, grad_out, out):
 
     with ExitStack() as ctx:
         rawp = ctx.enter_context(tc.tile_pool(name="rawp", bufs=4))
-        grpp = ctx.enter_context(tc.tile_pool(name="grpp", bufs=3))
+        grpp = ctx.enter_context(tc.tile_pool(name="grpp", bufs=4))
         keep = ctx.enter_context(tc.tile_pool(name="keep", bufs=1))
-        lpool = ctx.enter_context(tc.tile_pool(name="lpool", bufs=4))
+        lpool = ctx.enter_context(tc.tile_pool(name="lpool", bufs=3))
         epool = ctx.enter_context(tc.tile_pool(name="epool", bufs=3))
         tpool = ctx.enter_context(tc.tile_pool(name="tpool", bufs=3))
         small = ctx.enter_context(tc.tile_pool(name="small", bufs=4))
@@ -163,6 +163,16 @@ def tile_spatialgather_module_kernel(tc, feats, probs, grad_out, out):
                 out=grp[i][:].rearrange("p (c i) t -> p c t i", i=4),
                 in_=raw[i][:].rearrange("p t (c i) -> p c t i", i=4),
             )
+
+        def rgg(i):
+            grp[i] = grpp.tile([P, CH, PACK], BF16, name="grp", tag="grp", align_bytes=64)
+            for a in range(0, CH, CH // 4):
+                e = a + CH // 4
+                nc.gpsimd.tensor_scalar(
+                    out=grp[i][:, a:e].rearrange("p (c i) t -> p c t i", i=4),
+                    in0=raw[i][:, :, a:e].rearrange("p t (c i) -> p c t i", i=4),
+                    scalar1=1.0, scalar2=0.0, op0=ALU.mult, op1=ALU.add,
+                )
 
         def q(i):
             if ITEMS[i][0] == "g":
@@ -278,7 +288,7 @@ def tile_spatialgather_module_kernel(tc, feats, probs, grad_out, out):
             nc.sync.dma_start(out=o_v[b, kt][:, lo:hi], in_=tt[t][:, lo:hi])
 
         ops = {
-            "ld_raw": ld_raw, "ld_l": ld_l, "warm": warm, "rg": rg, "q": q, "mx": mx, "ex": ex, "rc": rc,
+            "ld_raw": ld_raw, "ld_l": ld_l, "warm": warm, "rg": rg, "rgg": rgg, "q": q, "mx": mx, "ex": ex, "rc": rc,
             "mm": mm, "p1": p1, "c2": c2f, "p2v": p2v, "u": u, "p2g": p2g, "st": st, "dg": dgf, "pma": pma, "pmb": pmb, "pe": pe,
         }
         with tc.manual_schedule():

@@ -28,13 +28,14 @@ NB = N // BANK
 GSTEP = 512
 USTEP = 512
 VPIECES = {2048: [(0, 768), (768, 1408), (1408, 2048)], 1280: [(0, 480), (480, 880), (880, 1280)]}
-TCOLS = {3: (1280, 2304), 4: (1280, 2304), 5: (1280, 2304), 6: (1280, 2304), 7: (0, 1024)}
+TCOLS = {3: (1024, 2048), 4: (1024, 2048), 5: (1280, 2304), 6: (1280, 2304), 7: (0, 1024)}
 LASTV = [(1024, 1536), (1536, 2304), (2304, 3200), (3200, 4096)]
 LSPLIT = {0: 2}
+GPC = 8
 NPRE = 6
 ITEMS = [("g", 0, 0, 128), ("x", 0, 0), ("x", 0, 1), ("x", 0, 2), ("x", 0, 3), ("g", 1, 0, 512), ("x", 1, 0), ("x", 1, 1), ("x", 1, 2), ("x", 1, 3), ("g", 0, 128, 512)]
-VCOLS = [2048, 2048, 2048, 1280, 1280, 1280, 1280, 4096]
-GLO = [2048, 2048, 2048, 2304, 2304, 2304, 2304, 4096]
+VCOLS = [2048, 2048, 2048, 1024, 1024, 1280, 1280, 4096]
+GLO = [2048, 2048, 2048, 2048, 2048, 2304, 2304, 4096]
 NGP = [4] * 7 + [1]
 
 
@@ -52,7 +53,7 @@ def build_order():
     s_extra = {0: [("ex", 3), ("rg", 8, "s")], 1: [("rg", 9, "s"), ("ex", 4)], 2: [("ex", 5)], 3: [("ex", 6)], 4: [("ex", 7)]}
     q_extra = {0: [("q", 6)], 1: [("q", 7), ("q", 5)], 2: [("q", 8), ("q", 9)]}
     v_extra = {0: [("mx", 4)], 1: [("mx", 5)], 2: [("mx", 6)], 3: [("mx", 7)]}
-    l_extra = {0: [("ld_l", 6)], 1: [("ld_l", 7)]}
+    l_extra = {0: [("ld_l", 6)], 2: [("ld_l", 7)]}
     for t in range(NT - 1):
         n = t + 1
         if t not in TCOLS:
@@ -166,8 +167,8 @@ def tile_spatialgather_module_kernel(tc, feats, probs, grad_out, out):
 
         def rgg(i):
             grp[i] = grpp.tile([P, CH, PACK], BF16, name="grp", tag="grp", align_bytes=64)
-            for a in range(0, CH, CH // 4):
-                e = a + CH // 4
+            for a in range(0, CH, CH // GPC):
+                e = a + CH // GPC
                 nc.gpsimd.tensor_scalar(
                     out=grp[i][:, a:e].rearrange("p (c i) t -> p c t i", i=4),
                     in0=raw[i][:, :, a:e].rearrange("p t (c i) -> p c t i", i=4),

from contextlib import ExitStack

import concourse.mybir as mybir
from concourse.masks import make_identity

FLOPS = 2 * 2 * 512 * 512 * 4096

F32 = mybir.dt.float32
BF16 = mybir.dt.bfloat16
U32 = mybir.dt.uint32
U8 = mybir.dt.uint8
E4X4 = mybir.dt.float8_e4m3fn_x4
E5X4 = mybir.dt.float8_e5m2_x4
ALU = mybir.AluOpType
ACT = mybir.ActivationFunctionType

P = 128
PACK = 4
B = 2
K = 512
N = 4096
KT = K // P
NT = B * KT
CH = 1024
NCH = N // CH
BANK = 512
NB = N // BANK
GSTEP = 512
USTEP = 512
VPIECES = {2048: [(0, 768), (768, 1408), (1408, 2048)], 1280: [(0, 480), (480, 880), (880, 1280)]}
TCOLS = {3: (1024, 2048), 4: (1024, 2048), 5: (1280, 2304), 6: (1280, 2304), 7: (0, 1024)}
LASTV = [(1024, 1536), (1536, 2304), (2304, 3200), (3200, 4096)]
LSPLIT = {0: 2}
GPC = 8
NPRE = 6
ITEMS = [("g", 0, 0, 128), ("x", 0, 0), ("x", 0, 1), ("x", 0, 2), ("x", 0, 3), ("g", 1, 0, 512), ("x", 1, 0), ("x", 1, 1), ("x", 1, 2), ("x", 1, 3), ("g", 0, 128, 512)]
VCOLS = [2048, 2048, 2048, 1024, 1024, 1280, 1280, 4096]
GLO = [2048, 2048, 2048, 2048, 2048, 2304, 2304, 4096]
NGP = [4] * 7 + [1]


def build_order():
    seq = []
    seq += [("ld_l", 0), ("ld_raw", 0), ("ld_l", 1), ("ld_raw", 1), ("ld_raw", 2), ("warm",)]
    seq += [("mx", 0), ("ex", 0), ("rg", 0, "v"), ("ld_raw", 3), ("ld_raw", 4), ("ld_raw", 10), ("q", 0), ("mx", 1), ("ex", 1)]
    seq += [("rg", 1, "v"), ("ld_l", 2), ("ld_raw", 6), ("rg", 2, "v"), ("ld_l", 3), ("ld_raw", 7), ("q", 1), ("rg", 3, "s"), ("rg", 4, "s"), ("rc", 0), ("q", 2)]
    seq += [("mm", 0, 0), ("mm", 0, 1), ("mm", 0, 2), ("mm", 0, 3)]
    seq += [("p1", 0, 0), ("p1", 0, 1), ("p1", 0, 2), ("p1", 0, 3), ("rg", 10, "v"), ("rgg", 6), ("q", 3), ("mm", 0, 4), ("mm", 0, 5), ("q", 10)]
    seq += [("mx", 2), ("ex", 2), ("ld_raw", 8), ("ld_l", 4), ("p1", 0, 4), ("q", 4), ("p1", 0, 5), ("rc", 1), ("ld_raw", 5), ("ld_l", 5)]
    seq += [("mm", 0, 6), ("mm", 0, 7)]
    seq += [("p1", 0, 6), ("p1", 0, 7)]
    seq += [("ld_raw", 9), ("c2", 0), ("mx", 3), ("u", 0), ("rg", 7, "s"), ("rg", 5, "s")]
    s_extra = {0: [("ex", 3), ("rg", 8, "s")], 1: [("rg", 9, "s"), ("ex", 4)], 2: [("ex", 5)], 3: [("ex", 6)], 4: [("ex", 7)]}
    q_extra = {0: [("q", 6)], 1: [("q", 7), ("q", 5)], 2: [("q", 8), ("q", 9)]}
    v_extra = {0: [("mx", 4)], 1: [("mx", 5)], 2: [("mx", 6)], 3: [("mx", 7)]}
    l_extra = {0: [("ld_l", 6)], 2: [("ld_l", 7)]}
    for t in range(NT - 1):
        n = t + 1
        if t not in TCOLS:
            seq += [("mm", n, j) for j in range(NB)]
        seq += [("p1", n, j) for j in range(NB)]
        seq += [("p2g", t)]
        if t < 6:
            seq += [("st", t, GLO[t], 4096)]
        if t in TCOLS:
            seq += [("st", t, TCOLS[t][0], TCOLS[t][1])]
        pcs = [(c, c + BANK) for c in range(TCOLS[n][0], TCOLS[n][1], BANK)] if n in TCOLS else []
        if pcs:
            if n + 1 < NT and n != KT - 1:
                seq += [("mm", n + 1, j) for j in range(NPRE)]
            seq += [("pma", n, c) for c, e in pcs]
        if t < NT - 2:
            seq += [("p2v", t, 0), ("st", t, 0, VCOLS[t])] + q_extra.get(t, [])
        if t not in v_extra and n + 1 < NT:
            seq += [("rc", n + 1)]
        seq += [("c2", n)]
        if t in v_extra:
            seq += [("rc", n + 1)] + v_extra[t]
        if n == NT - 2:
            seq += [("p2v", n, 0), ("st", n, 0, VCOLS[n])]
        if pcs:
            if n + 1 < NT:
                seq += [("mm", n + 1, j) for j in range(NPRE if n != KT - 1 else 0, NB)]
            seq += [("dg", n)] + [("pmb", n, c) for c, e in pcs]
        seq += [("u", n)] + s_extra.get(t, [])
        if pcs:
            seq += [("pe", n, c) for c, e in pcs]
        seq += l_extra.get(t, [])
    for h in range(len(LASTV)):
        seq += [("p2v", NT - 1, h), ("st", NT - 1, LASTV[h][0], LASTV[h][1])]
        if 0 < h < 3:
            seq += [("st", NT - 1, (h - 1) * BANK, h * BANK)]
    return seq


def tile_spatialgather_module_kernel(tc, feats, probs, grad_out, out):
    nc = tc.nc
    x_v = feats.rearrange("b (p j) h w -> b p j (h w)", j=PACK)
    g_v = grad_out.rearrange("b (p j) k o -> p b j (k o)", j=PACK)
    l_v = probs.rearrange("b (t p) h w -> b t p (h w)", p=P)
    o_v = out.rearrange("b (t p) h w -> b t p (h w)", p=P)

    with ExitStack() as ctx:
        rawp = ctx.enter_context(tc.tile_pool(name="rawp", bufs=4))
        grpp = ctx.enter_context(tc.tile_pool(name="grpp", bufs=4))
        keep = ctx.enter_context(tc.tile_pool(name="keep", bufs=1))
        lpool = ctx.enter_context(tc.tile_pool(name="lpool", bufs=3))
        epool = ctx.enter_context(tc.tile_pool(name="epool", bufs=3))
        tpool = ctx.enter_context(tc.tile_pool(name="tpool", bufs=3))
        small = ctx.enter_context(tc.tile_pool(name="small", bufs=4))
        psum = ctx.enter_context(tc.psum_pool(name="psum", bufs=6))
        psadd = ctx.enter_context(tc.psum_pool(name="psadd", bufs=2))
        dgp = ctx.enter_context(tc.tile_pool(name="dgp", bufs=2))

        g_codes = keep.tile([P, B * K], U32, name="g_codes", align_bytes=64)
        g_scales = keep.tile([P, B * K], U8, name="g_scales", align_bytes=64)
        x_codes = [keep.tile([P, N], U32, name="x_codes%d" % b, align_bytes=64) for b in range(B)]
        x_scales = [keep.tile([P, N], U8, name="x_scales%d" % b, align_bytes=64) for b in range(B)]

        ident = keep.tile([P, P], F32, name="ident")
        make_identity(nc, ident[:])
        dgt = {}
        pp = {}
        raw = {}
        grp = {}
        lt = {}
        et = {}
        tt = {}
        ps = {}
        negm = {}
        ssum = {}
        rs = {}
        dparts = {}
        c2 = {}

        def ld_raw(i):
            if ITEMS[i][0] == "g":
                kind, b, lo, hi = ITEMS[i]
                raw[i] = rawp.tile([P, PACK, hi - lo], BF16, name="raw", tag="raw")
                nc.sync.dma_start(out=raw[i][:], in_=g_v[:, b, :, lo:hi])
            else:
                kind, b, c = ITEMS[i]
                raw[i] = rawp.tile([P, PACK, CH], BF16, name="raw", tag="raw")
                nc.sync.dma_start(out=raw[i][:], in_=x_v[b, :, :, c * CH : (c + 1) * CH])

        def ld_l(t):
            b, kt = divmod(t, KT)
            lt[t] = lpool.tile([P, N], BF16, name="lt", tag="lt")
            for lo in range(0, N, N // LSPLIT.get(t, 1)):
                hi = lo + N // LSPLIT.get(t, 1)
                nc.sync.dma_start(out=lt[t][:, lo:hi], in_=l_v[b, kt][:, lo:hi])

        def warm():
            w0 = small.tile([P, 1], F32, name="w0", tag="w0")
            w1 = small.tile([P, 1], F32, name="w1", tag="w1")
            nc.vector.memset(w0[:], 0.0)
            nc.scalar.activation(out=w1[:], in_=w0[:], func=ACT.Exp)

        def rg(i, eng):
            copy = nc.vector.tensor_copy if eng == "v" else nc.scalar.copy
            width = ITEMS[i][3] - ITEMS[i][2] if ITEMS[i][0] == "g" else CH
            grp[i] = grpp.tile([P, width, PACK], BF16, name="grp", tag="grp", align_bytes=64)
            copy(
                out=grp[i][:].rearrange("p (c i) t -> p c t i", i=4),
                in_=raw[i][:].rearrange("p t (c i) -> p c t i", i=4),
            )

        def rgg(i):
            grp[i] = grpp.tile([P, CH, PACK], BF16, name="grp", tag="grp", align_bytes=64)
            for a in range(0, CH, CH // GPC):
                e = a + CH // GPC
                nc.gpsimd.tensor_scalar(
                    out=grp[i][:, a:e].rearrange("p (c i) t -> p c t i", i=4),
                    in0=raw[i][:, :, a:e].rearrange("p t (c i) -> p c t i", i=4),
                    scalar1=1.0, scalar2=0.0, op0=ALU.mult, op1=ALU.add,
                )

        def q(i):
            if ITEMS[i][0] == "g":
                kind, b, lo, hi = ITEMS[i]
                for a in [lo] if lo == 0 else [lo, 2 * lo]:
                    e = min(2 * a, hi) if lo else hi
                    nc.vector.quantize_mx(
                        out=g_codes[:, b * K + a : b * K + e].bitcast(E5X4),
                        scales=g_scales[:, b * K + a : b * K + e],
                        in_=grp[i][:, a - lo : e - lo].rearrange("p w j -> p (w j)"),
                    )
                return
            kind, b, c = ITEMS[i]
            nc.vector.quantize_mx(
                out=x_codes[b][:, c * CH : (c + 1) * CH].bitcast(E4X4),
                scales=x_scales[b][:, c * CH : (c + 1) * CH],
                in_=grp[i][:].rearrange("p w j -> p (w j)"),
            )

        def mx(t):
            start = None
            for lo in range(0, N, N // LSPLIT.get(t, 1)):
                hi = lo + N // LSPLIT.get(t, 1)
                negm[t] = small.tile([P, 1], F32, name="negm", tag="negm")
                nc.vector.tensor_scalar(
                    out=lt[t][:, lo:hi], in0=lt[t][:, lo:hi], scalar1=-1.0, scalar2=start,
                    op0=ALU.mult, op1=ALU.min, accum_out=negm[t][:],
                )
                start = negm[t][:]

        def ex(t):
            et[t] = epool.tile([P, N], F32, name="et", tag="et")
            ssum[t] = small.tile([P, 1], F32, name="ssum", tag="ssum")
            nc.scalar.activation(
                out=et[t][:], in_=lt[t][:], func=ACT.Exp, bias=negm[t][:], scale=-1.0, accum_out=ssum[t][:],
            )

        def rc(t):
            rs[t] = small.tile([P, 1], F32, name="rs", tag="rs")
            nc.vector.reciprocal(out=rs[t][:], in_=ssum[t][:])

        def mm(t, j):
            b, kt = divmod(t, KT)
            ps[(t, j)] = psum.tile([P, BANK], F32, name="ps", tag="ps")
            gcols = slice(b * K + kt * P, b * K + (kt + 1) * P)
            xcols = slice(j * BANK, (j + 1) * BANK)
            nc.tensor.matmul_mx(
                out=ps[(t, j)][:],
                lhsT=g_codes[:, gcols].bitcast(E5X4),
                lhsT_scale=g_scales[:, gcols],
                rhs=x_codes[b][:, xcols].bitcast(E4X4),
                rhs_scale=x_scales[b][:, xcols],
                start=True,
                stop=True,
            )

        def p1(t, j):
            if j == 0:
                tt[t] = tpool.tile([P, N], F32, name="tt", tag="tt")
                dparts[t] = small.tile([P, NB], F32, name="dparts", tag="dparts")
            cols = slice(j * BANK, (j + 1) * BANK)
            nc.vector.scalar_tensor_tensor(
                out=tt[t][:, cols], in0=ps[(t, j)][:], scalar=rs[t][:], in1=et[t][:, cols],
                op0=ALU.mult, op1=ALU.mult, accum_out=dparts[t][:, j : j + 1],
            )

        def c2f(t):
            c2[t] = small.tile([P, 1], F32, name="c2", tag="c2")
            nc.vector.tensor_scalar(
                out=dparts[t][:], in0=dparts[t][:], scalar1=rs[t][:], scalar2=None,
                op0=ALU.mult, op1=ALU.subtract, accum_out=c2[t][:],
            )

        def p2v(t, h):
            lo, hi = (0, VCOLS[t]) if VCOLS[t] < N else LASTV[h]
            cols = slice(lo, hi)
            nc.vector.scalar_tensor_tensor(
                out=tt[t][:, cols], in0=et[t][:, cols], scalar=c2[t][:], in1=tt[t][:, cols],
                op0=ALU.mult, op1=ALU.add,
            )

        def u(t):
            for c0 in range(GLO[t], N, max((N - GLO[t]) // NGP[t], 1)):
                cols = slice(c0, c0 + (N - GLO[t]) // NGP[t])
                nc.scalar.activation(out=et[t][:, cols], in_=et[t][:, cols], func=ACT.Copy, scale=c2[t][:])

        def p2g(t):
            for c0 in range(GLO[t], N, max((N - GLO[t]) // NGP[t], 1)):
                cols = slice(c0, c0 + (N - GLO[t]) // NGP[t])
                nc.gpsimd.tensor_tensor(out=tt[t][:, cols], in0=tt[t][:, cols], in1=et[t][:, cols], op=ALU.add)
                if t >= 6:
                    st(t, cols.start, cols.stop)

        def dgf(t):
            dgt[t] = dgp.tile([P, P], F32, name="dgt", tag="dgt")
            nc.scalar.activation(out=dgt[t][:], in_=ident[:], func=ACT.Copy, scale=c2[t][:])

        def pma(t, c0):
            if t == NT - 1:
                pp[(t, c0)] = psum.tile([P, BANK], F32, name="ps", tag="ps")
            else:
                pp[(t, c0)] = psadd.tile([P, BANK], F32, name="pp", tag="pp")
            nc.tensor.matmul(out=pp[(t, c0)][:], lhsT=ident[:], rhs=tt[t][:, c0 : c0 + BANK], start=True, stop=False)

        def pmb(t, c0):
            nc.tensor.matmul(out=pp[(t, c0)][:], lhsT=dgt[t][:], rhs=et[t][:, c0 : c0 + BANK], start=False, stop=True)

        def pe(t, c0):
            nc.scalar.copy(out=tt[t][:, c0 : c0 + BANK], in_=pp[(t, c0)][:])

        def st(t, lo, hi):
            b, kt = divmod(t, KT)
            nc.sync.dma_start(out=o_v[b, kt][:, lo:hi], in_=tt[t][:, lo:hi])

        ops = {
            "ld_raw": ld_raw, "ld_l": ld_l, "warm": warm, "rg": rg, "rgg": rgg, "q": q, "mx": mx, "ex": ex, "rc": rc,
            "mm": mm, "p1": p1, "c2": c2f, "p2v": p2v, "u": u, "p2g": p2g, "st": st, "dg": dgf, "pma": pma, "pmb": pmb, "pe": pe,
        }
        with tc.manual_schedule():
            for step in build_order():
                ops[step[0]](*step[1:])
